import numpy as np
import ml_dtypes


def mxq(x, axis, fmt="e4m3"):
    dtype, down = {"e4m3": (ml_dtypes.float8_e4m3fn, 7), "e5m2": (ml_dtypes.float8_e5m2, 14)}[fmt]
    v = np.moveaxis(np.asarray(x, np.float32).astype(ml_dtypes.bfloat16).astype(np.float64), axis, -1)
    blocks = v.reshape(v.shape[:-1] + (-1, 32))
    amax = np.abs(blocks).max(-1, keepdims=True)
    byte = np.maximum(np.where(amax > 0, np.frexp(amax)[1] - 1 + 127, 0) - down, 1)
    scale = np.exp2(byte - 127.0)
    codes = (blocks / scale).astype(np.float32).astype(dtype).astype(np.float64)
    return np.moveaxis((codes * scale).reshape(v.shape), -1, axis)


WIDE = False


def mx_kscale(k):
    if not WIDE:
        return np.ones(k)
    levels = np.array([10, -10, 5, -5, 0])
    a = np.random.permutation(np.resize(levels, k // 512 * 4)).reshape(k // 512, 4)
    idx = np.arange(k)
    return np.exp2(a[idx // 512, idx % 128 // 32])


BF16 = ml_dtypes.bfloat16


def bf(x):
    return np.asarray(x, np.float32).astype(BF16)


def f64(x):
    return np.asarray(x).astype(np.float64)


B, IN, OUT = 2048, 1024, 1024
MU = 0.25


def setup_inputs():
    s = mx_kscale(IN)
    x = np.random.standard_normal((B, IN)) + MU * np.random.standard_normal(IN)
    return {"x": bf(x * s),
            "wa": bf(np.random.standard_normal((OUT, IN)) / MU / s),
            "wb": bf(np.random.standard_normal((OUT, IN)) / MU),
            "wc": bf(np.random.standard_normal((OUT, IN)) * 12.0 / s),
            "wd": bf(np.random.standard_normal((OUT, IN))),
            "weight": bf(np.random.standard_normal((OUT, IN)) / np.sqrt(IN) / s)}


def reference(x, wa, wb, wc, wd, weight):
    x_ = f64(x)
    y_ = mxq(x_, 1, "e4m3") @ mxq(f64(weight), 1, "e4m3").T
    corr = mxq(y_, 0, "e4m3").T @ mxq(x_, 0, "e4m3")
    dw = (x_.mean(axis=0)[None, :] * f64(wa)
          + y_.mean(axis=0)[:, None] * f64(wb)
          + corr * f64(wc) / B
          + f64(wd))
    return dw

@@ -1,0 +1,231 @@
+import concourse.mybir as mybir
+from concourse.masks import make_identity
+
+F32 = mybir.dt.float32
+BF16 = mybir.dt.bfloat16
+U32 = mybir.dt.uint32
+U8 = mybir.dt.uint8
+FP8X4 = mybir.dt.float8_e4m3fn_x4
+ALU = mybir.AluOpType
+ACT = mybir.ActivationFunctionType
+
+P = 128
+PACK = 4
+K_PASS = P * PACK
+BANK = 512
+
+B, IN, OUT = 2048, 1024, 1024
+GROUPS = B // K_PASS
+IN_PASSES = IN // K_PASS
+OUT_TILES = OUT // P
+HALVES = IN // BANK
+
+FLOPS = 2 * B * IN * OUT * 2
+
+
+def tile_hebbianlinear_pa_kernel(tc, x, wa, wb, wc, wd, weight, out):
+    nc = tc.nc
+
+    with (
+        tc.tile_pool(name="keep", bufs=1) as keep,
+        tc.tile_pool(name="stage", bufs=4) as stage,
+        tc.tile_pool(name="work", bufs=2) as work,
+        tc.tile_pool(name="result", bufs=3) as result,
+        tc.psum_pool(name="psum_wide", bufs=4) as psum_wide,
+        tc.psum_pool(name="psum_flip", bufs=2) as psum_flip,
+        tc.psum_pool(name="psum_sum", bufs=2) as psum_sum,
+    ):
+        x_rows = x.rearrange("(g p t) k -> g p (t k)", p=P, t=PACK)
+        x_sb = [keep.tile([P, PACK * IN], BF16, name="x_sb%d" % g) for g in range(GROUPS)]
+        w_sb = keep.tile([P, OUT_TILES * IN], BF16)
+        wa_sb = keep.tile([P, OUT_TILES, IN], BF16)
+        wb_sb = keep.tile([P, OUT_TILES, IN], BF16)
+        wc_sb = keep.tile([P, OUT_TILES, IN], BF16)
+        wd_sb = keep.tile([P, OUT_TILES, IN], BF16)
+        nc.sync.dma_start(out=x_sb[0][:], in_=x_rows[0])
+        nc.sync.dma_start(out=w_sb[:], in_=weight.rearrange("(p ot) k -> p (ot k)", ot=OUT_TILES))
+        for g in range(1, GROUPS):
+            nc.sync.dma_start(out=x_sb[g][:], in_=x_rows[g])
+        for sb, dram in ((wa_sb, wa), (wd_sb, wd), (wb_sb, wb), (wc_sb, wc)):
+            nc.sync.dma_start(out=sb[:], in_=dram.rearrange("(p ot) i -> p ot i", ot=OUT_TILES))
+        out_tiles = out.rearrange("(p ot) i -> p ot i", ot=OUT_TILES)
+
+        ident_f32 = keep.tile([P, P], F32)
+        make_identity(nc, ident_f32[:])
+        ident_bf16 = keep.tile([P, P], BF16)
+        make_identity(nc, ident_bf16[:])
+        one_over_b = keep.tile([P, P], BF16)
+        nc.vector.memset(one_over_b[:], 1.0 / B)
+
+        xk_codes = keep.tile([P, IN_PASSES, GROUPS, K_PASS], U32, align_bytes=64)
+        xk_scales = keep.tile([P, IN_PASSES, GROUPS, K_PASS], U8, align_bytes=64)
+        wk_codes = keep.tile([P, IN_PASSES, OUT], U32, align_bytes=64)
+        wk_scales = keep.tile([P, IN_PASSES, OUT], U8, align_bytes=64)
+        xb_codes = keep.tile([P, GROUPS, IN], U32, align_bytes=64)
+        xb_scales = keep.tile([P, GROUPS, IN], U8, align_bytes=64)
+
+        def quantise_along_features(rows_sb, c, codes, scales):
+            words = rows_sb.bitcast(F32).rearrange("p (s w) -> p s w", s=PACK)
+            grouped = stage.tile([P, PACK * K_PASS], BF16, tag="grouped", align_bytes=64)
+            grouped_words = grouped[:].bitcast(F32).rearrange("p (s r u) -> p s r u", s=PACK, u=2)
+            for pair in range(2):
+                flipped = psum_wide.tile([P, 2, 2, P], F32, tag="wide")
+                for u in range(2):
+                    for s in range(2):
+                        first = (K_PASS // 2) * c + P * u
+                        nc.tensor.transpose(
+                            out=flipped[:, u, s, :],
+                            in_=words[:, 2 * pair + s, first : first + P],
+                            identity=ident_f32[:],
+                        )
+                nc.scalar.copy(
+                    out=grouped_words[:, 2 * pair : 2 * pair + 2, :, :],
+                    in_=flipped[:].rearrange("p u s r -> p s r u"),
+                )
+            nc.vector.quantize_mx(out=codes.bitcast(FP8X4), scales=scales, in_=grouped[:])
+
+        def quantise_x_along_batch(g, h, copy):
+            rows = x_sb[g][:].rearrange("p (t i) -> p t i", t=PACK)[:, :, BANK * h : BANK * (h + 1)]
+            grouped = stage.tile([P, PACK * BANK], BF16, tag="grouped", align_bytes=64)
+            copy(
+                out=grouped[:].rearrange("p (n i t) -> p n t i", i=4, t=PACK),
+                in_=rows.rearrange("p t (n i) -> p n t i", i=4),
+            )
+            cols = slice(BANK * h, BANK * (h + 1))
+            nc.vector.quantize_mx(
+                out=xb_codes[:, g, cols].bitcast(FP8X4), scales=xb_scales[:, g, cols], in_=grouped[:]
+            )
+
+        xm_ps = [psum_sum.tile([P, BANK], F32, tag="sum", name="xm_ps%d" % h) for h in range(HALVES)]
+
+        def add_to_xm(g):
+            for t in range(PACK):
+                for h in range(HALVES):
+                    first = IN * t + BANK * h
+                    nc.tensor.matmul(
+                        out=xm_ps[h][:],
+                        lhsT=one_over_b[:],
+                        rhs=x_sb[g][:, first : first + BANK],
+                        start=(g == 0 and t == 0),
+                        stop=(g == GROUPS - 1 and t == PACK - 1),
+                    )
+
+        def prepare_x(g):
+            for c in range(IN_PASSES):
+                quantise_along_features(x_sb[g][:], c, xk_codes[:, c, g, :], xk_scales[:, c, g, :])
+            add_to_xm(g)
+
+        prepare_x(0)
+        for four in range(OUT_TILES // PACK):
+            rows = w_sb[:, PACK * IN * four : PACK * IN * (four + 1)]
+            cols = slice(K_PASS * four, K_PASS * (four + 1))
+            for c in range(IN_PASSES):
+                quantise_along_features(rows, c, wk_codes[:, c, cols], wk_scales[:, c, cols])
+        for g in range(1, GROUPS):
+            prepare_x(g)
+
+        xm_all = keep.tile([P, IN], F32)
+        for h in range(HALVES):
+            nc.vector.tensor_copy(out=xm_all[:, BANK * h : BANK * (h + 1)], in_=xm_ps[h][:])
+
+        for g in range(GROUPS):
+            quantise_x_along_batch(g, 0, nc.vector.tensor_copy)
+            quantise_x_along_batch(g, 1, nc.scalar.copy)
+
+        y_sums = keep.tile([P, OUT_TILES, GROUPS], F32)
+        ym = keep.tile([P, OUT_TILES], F32)
+        yT_sb = {}
+        y_codes = {}
+        y_scales = {}
+        base = {}
+
+        def first_matmul(ot):
+            yT_sb[ot] = work.tile([P, GROUPS, K_PASS], BF16, tag="yT", name="yT%d" % ot)
+            w_cols = slice(P * ot, P * (ot + 1))
+            for g in range(GROUPS):
+                yT_ps = psum_wide.tile([P, BANK], F32, tag="wide")
+                for c in range(IN_PASSES):
+                    nc.tensor.matmul_mx(
+                        out=yT_ps[:],
+                        lhsT=wk_codes[:, c, w_cols].bitcast(FP8X4),
+                        lhsT_scale=wk_scales[:, c, w_cols],
+                        rhs=xk_codes[:, c, g, :].bitcast(FP8X4),
+                        rhs_scale=xk_scales[:, c, g, :],
+                        start=(c == 0),
+                        stop=(c == IN_PASSES - 1),
+                    )
+                nc.scalar.activation(
+                    out=yT_sb[ot][:, g, :], in_=yT_ps[:], func=ACT.Copy, accum_out=y_sums[:, ot, g : g + 1]
+                )
+            scaled = work.tile([P, GROUPS], F32, tag="scaled")
+            nc.scalar.activation(
+                out=scaled[:], in_=y_sums[:, ot, :], func=ACT.Copy, scale=1.0 / B, accum_out=ym[:, ot : ot + 1]
+            )
+
+        def quantise_y(ot):
+            grouped = work.tile([P, GROUPS, P, PACK], BF16, tag="y_grouped", align_bytes=64)
+            for pair in range(GROUPS // 2):
+                flipped = psum_flip.tile([P, 2, PACK, P], BF16, tag="flip")
+                for g in range(2):
+                    for t in range(PACK):
+                        nc.tensor.transpose(
+                            out=flipped[:, g, t, :],
+                            in_=yT_sb[ot][:, 2 * pair + g, P * t : P * (t + 1)],
+                            identity=ident_bf16[:],
+                        )
+                nc.scalar.copy(
+                    out=grouped[:, 2 * pair : 2 * pair + 2, :, :],
+                    in_=flipped[:].rearrange("p g t o -> p g o t"),
+                )
+            y_codes[ot] = work.tile([P, GROUPS * P], U32, tag="y_codes", name="y_codes%d" % ot, align_bytes=64)
+            y_scales[ot] = work.tile([P, GROUPS * P], U8, tag="y_scales", name="y_scales%d" % ot, align_bytes=64)
+            nc.vector.quantize_mx(
+                out=y_codes[ot][:].bitcast(FP8X4),
+                scales=y_scales[ot][:],
+                in_=grouped[:].rearrange("p g o t -> p (g o t)"),
+            )
+
+        def terms_without_second_matmul(ot):
+            base[ot] = result.tile([P, IN], F32, tag="base", name="base%d" % ot)
+            nc.vector.tensor_tensor(out=base[ot][:], in0=wa_sb[:, ot, :], in1=xm_all[:], op=ALU.mult)
+            nc.vector.tensor_tensor(out=base[ot][:], in0=base[ot][:], in1=wd_sb[:, ot, :], op=ALU.add)
+            nc.vector.scalar_tensor_tensor(
+                out=base[ot][:],
+                in0=wb_sb[:, ot, :],
+                scalar=ym[:, ot : ot + 1],
+                in1=base[ot][:],
+                op0=ALU.mult,
+                op1=ALU.add,
+            )
+
+        def second_matmul(ot):
+            for h in range(HALVES):
+                cols = slice(BANK * h, BANK * (h + 1))
+                corr_ps = psum_sum.tile([P, BANK], F32, tag="sum")
+                for g in range(GROUPS):
+                    y_cols = slice(P * g, P * (g + 1))
+                    nc.tensor.matmul_mx(
+                        out=corr_ps[:],
+                        lhsT=y_codes[ot][:, y_cols].bitcast(FP8X4),
+                        lhsT_scale=y_scales[ot][:, y_cols],
+                        rhs=xb_codes[:, g, cols].bitcast(FP8X4),
+                        rhs_scale=xb_scales[:, g, cols],
+                        start=(g == 0),
+                        stop=(g == GROUPS - 1),
+                    )
+                hebb = work.tile([P, BANK], F32, tag="hebb")
+                nc.vector.scalar_tensor_tensor(
+                    out=hebb[:], in0=corr_ps[:], scalar=1.0 / B, in1=wc_sb[:, ot, cols], op0=ALU.mult, op1=ALU.mult
+                )
+                nc.vector.tensor_tensor(out=base[ot][:, cols], in0=hebb[:], in1=base[ot][:, cols], op=ALU.add)
+                nc.sync.dma_start(out=out_tiles[:, ot, cols], in_=base[ot][:, cols])
+
+        first_matmul(0)
+        for ot in range(OUT_TILES):
+            quantise_y(ot)
+            if ot + 1 < OUT_TILES:
+                first_matmul(ot + 1)
+            terms_without_second_matmul(ot)
+            if ot >= 1:
+                second_matmul(ot - 1)
+        second_matmul(OUT_TILES - 1)

@@ -28,7 +28,7 @@ def tile_hebbianlinear_pa_kernel(tc, x, wa, wb, wc, wd, weight, out):
 
     with (
         tc.tile_pool(name="keep", bufs=1) as keep,
-        tc.tile_pool(name="stage", bufs=4) as stage,
+        tc.tile_pool(name="stage", bufs=3) as stage,
         tc.tile_pool(name="work", bufs=2) as work,
         tc.tile_pool(name="result", bufs=3) as result,
         tc.psum_pool(name="psum_wide", bufs=4) as psum_wide,
@@ -46,8 +46,11 @@ def tile_hebbianlinear_pa_kernel(tc, x, wa, wb, wc, wd, weight, out):
         nc.sync.dma_start(out=w_sb[:], in_=weight.rearrange("(p ot) k -> p (ot k)", ot=OUT_TILES))
         for g in range(1, GROUPS):
             nc.sync.dma_start(out=x_sb[g][:], in_=x_rows[g])
-        for sb, dram in ((wa_sb, wa), (wd_sb, wd), (wb_sb, wb), (wc_sb, wc)):
-            nc.sync.dma_start(out=sb[:], in_=dram.rearrange("(p ot) i -> p ot i", ot=OUT_TILES))
+        for tiles in (slice(0, OUT_TILES // 2), slice(OUT_TILES // 2, OUT_TILES)):
+            for sb, dram in ((wa_sb, wa), (wd_sb, wd), (wb_sb, wb), (wc_sb, wc)):
+                nc.sync.dma_start(
+                    out=sb[:, tiles, :], in_=dram.rearrange("(p ot) i -> p ot i", ot=OUT_TILES)[:, tiles, :]
+                )
         out_tiles = out.rearrange("(p ot) i -> p ot i", ot=OUT_TILES)
 
         ident_f32 = keep.tile([P, P], F32)
@@ -84,10 +87,10 @@ def tile_hebbianlinear_pa_kernel(tc, x, wa, wb, wc, wd, weight, out):
                 )
             nc.vector.quantize_mx(out=codes.bitcast(FP8X4), scales=scales, in_=grouped[:])
 
-        def quantise_x_along_batch(g, h, copy):
+        def quantise_x_along_batch(g, h):
             rows = x_sb[g][:].rearrange("p (t i) -> p t i", t=PACK)[:, :, BANK * h : BANK * (h + 1)]
-            grouped = stage.tile([P, PACK * BANK], BF16, tag="grouped", align_bytes=64)
-            copy(
+            grouped = stage.tile([P, PACK * BANK], BF16, tag="xb_grouped", bufs=2, align_bytes=64)
+            nc.vector.tensor_copy(
                 out=grouped[:].rearrange("p (n i t) -> p n t i", i=4, t=PACK),
                 in_=rows.rearrange("p t (n i) -> p n t i", i=4),
             )
@@ -113,6 +116,8 @@ def tile_hebbianlinear_pa_kernel(tc, x, wa, wb, wc, wd, weight, out):
         def prepare_x(g):
             for c in range(IN_PASSES):
                 quantise_along_features(x_sb[g][:], c, xk_codes[:, c, g, :], xk_scales[:, c, g, :])
+            for h in range(HALVES):
+                quantise_x_along_batch(g, h)
             add_to_xm(g)
 
         prepare_x(0)
@@ -126,11 +131,7 @@ def tile_hebbianlinear_pa_kernel(tc, x, wa, wb, wc, wd, weight, out):
 
         xm_all = keep.tile([P, IN], F32)
         for h in range(HALVES):
-            nc.vector.tensor_copy(out=xm_all[:, BANK * h : BANK * (h + 1)], in_=xm_ps[h][:])
-
-        for g in range(GROUPS):
-            quantise_x_along_batch(g, 0, nc.vector.tensor_copy)
-            quantise_x_along_batch(g, 1, nc.scalar.copy)
+            nc.scalar.copy(out=xm_all[:, BANK * h : BANK * (h + 1)], in_=xm_ps[h][:])
 
         y_sums = keep.tile([P, OUT_TILES, GROUPS], F32)
         ym = keep.tile([P, OUT_TILES], F32)
@@ -185,10 +186,12 @@ def tile_hebbianlinear_pa_kernel(tc, x, wa, wb, wc, wd, weight, out):
                 in_=grouped[:].rearrange("p g o t -> p (g o t)"),
             )
 
-        def terms_without_second_matmul(ot):
+        def start_base(ot):
             base[ot] = result.tile([P, IN], F32, tag="base", name="base%d" % ot)
             nc.vector.tensor_tensor(out=base[ot][:], in0=wa_sb[:, ot, :], in1=xm_all[:], op=ALU.mult)
             nc.vector.tensor_tensor(out=base[ot][:], in0=base[ot][:], in1=wd_sb[:, ot, :], op=ALU.add)
+
+        def finish_base(ot):
             nc.vector.scalar_tensor_tensor(
                 out=base[ot][:],
                 in0=wb_sb[:, ot, :],
@@ -221,11 +224,14 @@ def tile_hebbianlinear_pa_kernel(tc, x, wa, wb, wc, wd, weight, out):
                 nc.sync.dma_start(out=out_tiles[:, ot, cols], in_=base[ot][:, cols])
 
         first_matmul(0)
+        start_base(0)
         for ot in range(OUT_TILES):
             quantise_y(ot)
             if ot + 1 < OUT_TILES:
                 first_matmul(ot + 1)
-            terms_without_second_matmul(ot)
+            finish_base(ot)
+            if ot + 1 < OUT_TILES:
+                start_base(ot + 1)
             if ot >= 1:
                 second_matmul(ot - 1)
         second_matmul(OUT_TILES - 1)

@@ -13,6 +13,7 @@ P = 128
 PACK = 4
 K_PASS = P * PACK
 BANK = 512
+QUARTER = BANK // 2
 
 B, IN, OUT = 2048, 1024, 1024
 GROUPS = B // K_PASS
@@ -29,36 +30,57 @@ def tile_hebbianlinear_pa_kernel(tc, x, wa, wb, wc, wd, weight, out):
     with (
         tc.tile_pool(name="keep", bufs=1) as keep,
         tc.tile_pool(name="stage", bufs=3) as stage,
+        tc.tile_pool(name="slots", bufs=GROUPS) as slots,
         tc.tile_pool(name="work", bufs=2) as work,
-        tc.tile_pool(name="result", bufs=3) as result,
         tc.psum_pool(name="psum_wide", bufs=4) as psum_wide,
         tc.psum_pool(name="psum_flip", bufs=2) as psum_flip,
         tc.psum_pool(name="psum_sum", bufs=2) as psum_sum,
+        tc.manual_schedule(),
     ):
-        x_rows = x.rearrange("(g p t) k -> g p (t k)", p=P, t=PACK)
-        x_sb = [keep.tile([P, PACK * IN], BF16, name="x_sb%d" % g) for g in range(GROUPS)]
-        w_sb = keep.tile([P, OUT_TILES * IN], BF16)
-        wa_sb = keep.tile([P, OUT_TILES, IN], BF16)
-        wb_sb = keep.tile([P, OUT_TILES, IN], BF16)
-        wc_sb = keep.tile([P, OUT_TILES, IN], BF16)
-        wd_sb = keep.tile([P, OUT_TILES, IN], BF16)
-        nc.sync.dma_start(out=x_sb[0][:], in_=x_rows[0])
-        nc.sync.dma_start(out=w_sb[:], in_=weight.rearrange("(p ot) k -> p (ot k)", ot=OUT_TILES))
-        for g in range(1, GROUPS):
-            nc.sync.dma_start(out=x_sb[g][:], in_=x_rows[g])
-        for tiles in (slice(0, OUT_TILES // 2), slice(OUT_TILES // 2, OUT_TILES)):
-            for sb, dram in ((wa_sb, wa), (wd_sb, wd), (wb_sb, wb), (wc_sb, wc)):
-                nc.sync.dma_start(
-                    out=sb[:, tiles, :], in_=dram.rearrange("(p ot) i -> p ot i", ot=OUT_TILES)[:, tiles, :]
-                )
-        out_tiles = out.rearrange("(p ot) i -> p ot i", ot=OUT_TILES)
-
         ident_f32 = keep.tile([P, P], F32)
         make_identity(nc, ident_f32[:])
         ident_bf16 = keep.tile([P, P], BF16)
         make_identity(nc, ident_bf16[:])
-        one_over_b = keep.tile([P, P], BF16)
+        one_over_b = keep.tile([P, 1], BF16)
         nc.vector.memset(one_over_b[:], 1.0 / B)
+
+        x_rows = x.rearrange("(g p t) k -> g p t k", p=P, t=PACK)
+        x_sb = [slots.tile([P, PACK * IN], BF16, tag="slot", name="x_sb%d" % g) for g in range(GROUPS)]
+        w_sb = keep.tile([P, OUT_TILES, IN], BF16)
+        wa_sb = keep.tile([P, OUT_TILES, IN], BF16)
+        wb_sb = keep.tile([P, OUT_TILES, IN], BF16)
+        wc_sb = keep.tile([P, OUT_TILES, IN], BF16)
+        wd_sb = keep.tile([P, OUT_TILES, IN], BF16)
+
+        def load_x(g, cols):
+            nc.sync.dma_start(
+                out=x_sb[g][:].rearrange("p (t k) -> p t k", t=PACK)[:, :, cols], in_=x_rows[g][:, :, cols]
+            )
+
+        def load_tiles(sb, dram, half):
+            tiles = slice(PACK * half, PACK * (half + 1))
+            nc.sync.dma_start(
+                out=sb[:, tiles, :], in_=dram.rearrange("(p ot) i -> p ot i", ot=OUT_TILES)[:, tiles, :]
+            )
+
+        for h in range(HALVES):
+            load_x(0, slice(BANK * h, BANK * (h + 1)))
+        load_tiles(w_sb, weight, 0)
+        for g in range(1, GROUPS):
+            load_x(g, slice(0, IN))
+        for sb, dram, half in (
+            (wa_sb, wa, 0),
+            (wd_sb, wd, 0),
+            (w_sb, weight, 1),
+            (wb_sb, wb, 0),
+            (wc_sb, wc, 0),
+            (wa_sb, wa, 1),
+            (wd_sb, wd, 1),
+            (wb_sb, wb, 1),
+            (wc_sb, wc, 1),
+        ):
+            load_tiles(sb, dram, half)
+        out_tiles = out.rearrange("(p ot) i -> p ot i", ot=OUT_TILES)
 
         xk_codes = keep.tile([P, IN_PASSES, GROUPS, K_PASS], U32, align_bytes=64)
         xk_scales = keep.tile([P, IN_PASSES, GROUPS, K_PASS], U8, align_bytes=64)
@@ -67,7 +89,7 @@ def tile_hebbianlinear_pa_kernel(tc, x, wa, wb, wc, wd, weight, out):
         xb_codes = keep.tile([P, GROUPS, IN], U32, align_bytes=64)
         xb_scales = keep.tile([P, GROUPS, IN], U8, align_bytes=64)
 
-        def quantise_along_features(rows_sb, c, codes, scales):
+        def group_features(rows_sb, c):
             words = rows_sb.bitcast(F32).rearrange("p (s w) -> p s w", s=PACK)
             grouped = stage.tile([P, PACK * K_PASS], BF16, tag="grouped", align_bytes=64)
             grouped_words = grouped[:].bitcast(F32).rearrange("p (s r u) -> p s r u", s=PACK, u=2)
@@ -85,153 +107,272 @@ def tile_hebbianlinear_pa_kernel(tc, x, wa, wb, wc, wd, weight, out):
                     out=grouped_words[:, 2 * pair : 2 * pair + 2, :, :],
                     in_=flipped[:].rearrange("p u s r -> p s r u"),
                 )
-            nc.vector.quantize_mx(out=codes.bitcast(FP8X4), scales=scales, in_=grouped[:])
+            return grouped
 
-        def quantise_x_along_batch(g, h):
+        def quantise_x_features(g, c, grouped):
+            nc.vector.quantize_mx(
+                out=xk_codes[:, c, g, :].bitcast(FP8X4), scales=xk_scales[:, c, g, :], in_=grouped[:]
+            )
+
+        def quantise_weight(four):
+            cols = slice(K_PASS * four, K_PASS * (four + 1))
+            rows = w_sb[:, PACK * four : PACK * (four + 1), :].rearrange("p s k -> p (s k)")
+            grouped = [group_features(rows, c) for c in range(IN_PASSES)]
+            for c in range(IN_PASSES):
+                nc.vector.quantize_mx(
+                    out=wk_codes[:, c, cols].bitcast(FP8X4), scales=wk_scales[:, c, cols], in_=grouped[c][:]
+                )
+
+        def batch_tile():
+            return stage.tile([P, PACK * BANK], BF16, tag="xb_grouped", name="xb_grouped", bufs=2, align_bytes=64)
+
+        def group_batch_on_vector(g, h):
             rows = x_sb[g][:].rearrange("p (t i) -> p t i", t=PACK)[:, :, BANK * h : BANK * (h + 1)]
-            grouped = stage.tile([P, PACK * BANK], BF16, tag="xb_grouped", bufs=2, align_bytes=64)
+            grouped = batch_tile()
             nc.vector.tensor_copy(
                 out=grouped[:].rearrange("p (n i t) -> p n t i", i=4, t=PACK),
                 in_=rows.rearrange("p t (n i) -> p n t i", i=4),
             )
+            return grouped
+
+        def group_batch_on_scalar(g, h):
+            grouped = batch_tile()
+            for q in range(2):
+                bank = psum_flip.tile([P, PACK, QUARTER], BF16, tag="flip", name="rows_bank")
+                for t in range(PACK):
+                    first = IN * t + BANK * h + QUARTER * q
+                    nc.tensor.matmul(
+                        out=bank[:, t, :],
+                        lhsT=ident_bf16[:],
+                        rhs=x_sb[g][:, first : first + QUARTER],
+                        start=True,
+                        stop=True,
+                    )
+                nc.scalar.copy(
+                    out=grouped[:, PACK * QUARTER * q : PACK * QUARTER * (q + 1)].rearrange(
+                        "p (i t) -> p i t", t=PACK
+                    ),
+                    in_=bank[:].rearrange("p t i -> p i t"),
+                )
+            return grouped
+
+        def quantise_x_batch(g, h, grouped):
             cols = slice(BANK * h, BANK * (h + 1))
             nc.vector.quantize_mx(
                 out=xb_codes[:, g, cols].bitcast(FP8X4), scales=xb_scales[:, g, cols], in_=grouped[:]
             )
 
-        xm_ps = [psum_sum.tile([P, BANK], F32, tag="sum", name="xm_ps%d" % h) for h in range(HALVES)]
+        xm_ps = psum_sum.tile([P, GROUPS, IN // P], F32, tag="sum", name="xm_ps")
+        xm_col = keep.tile([P, IN // P], F32)
+        xm_all = keep.tile([P, IN], F32)
 
         def add_to_xm(g):
-            for t in range(PACK):
-                for h in range(HALVES):
-                    first = IN * t + BANK * h
+            for j in range(IN // P):
+                for t in range(PACK):
+                    first = IN * t + P * j
                     nc.tensor.matmul(
-                        out=xm_ps[h][:],
-                        lhsT=one_over_b[:],
-                        rhs=x_sb[g][:, first : first + BANK],
-                        start=(g == 0 and t == 0),
-                        stop=(g == GROUPS - 1 and t == PACK - 1),
+                        out=xm_ps[:, g, j : j + 1],
+                        lhsT=x_sb[g][:, first : first + P],
+                        rhs=one_over_b[:],
+                        start=(t == 0),
+                        stop=(t == PACK - 1),
                     )
 
-        def prepare_x(g):
-            for c in range(IN_PASSES):
-                quantise_along_features(x_sb[g][:], c, xk_codes[:, c, g, :], xk_scales[:, c, g, :])
+        def spread_xm():
             for h in range(HALVES):
-                quantise_x_along_batch(g, h)
-            add_to_xm(g)
-
-        prepare_x(0)
-        for four in range(OUT_TILES // PACK):
-            rows = w_sb[:, PACK * IN * four : PACK * IN * (four + 1)]
-            cols = slice(K_PASS * four, K_PASS * (four + 1))
-            for c in range(IN_PASSES):
-                quantise_along_features(rows, c, wk_codes[:, c, cols], wk_scales[:, c, cols])
-        for g in range(1, GROUPS):
-            prepare_x(g)
-
-        xm_all = keep.tile([P, IN], F32)
-        for h in range(HALVES):
-            nc.scalar.copy(out=xm_all[:, BANK * h : BANK * (h + 1)], in_=xm_ps[h][:])
+                spread = psum_sum.tile([P, BANK], F32, tag="sum", name="spread%d" % h)
+                for j in range(BANK // P):
+                    col = (BANK // P) * h + j
+                    nc.tensor.transpose(
+                        out=spread[:, P * j : P * (j + 1)],
+                        in_=xm_col[:, col : col + 1].to_broadcast([P, P]),
+                        identity=ident_f32[:],
+                    )
+                nc.scalar.copy(out=xm_all[:, BANK * h : BANK * (h + 1)], in_=spread[:])
 
         y_sums = keep.tile([P, OUT_TILES, GROUPS], F32)
         ym = keep.tile([P, OUT_TILES], F32)
         yT_sb = {}
+        y_grouped = {}
         y_codes = {}
         y_scales = {}
         base = {}
+        hebb = {}
 
-        def first_matmul(ot):
-            yT_sb[ot] = work.tile([P, GROUPS, K_PASS], BF16, tag="yT", name="yT%d" % ot)
+        def first_matmul(ot, g):
+            if g == 0:
+                yT_sb[ot] = work.tile([P, GROUPS, K_PASS], BF16, tag="yT", name="yT%d" % ot)
             w_cols = slice(P * ot, P * (ot + 1))
-            for g in range(GROUPS):
-                yT_ps = psum_wide.tile([P, BANK], F32, tag="wide")
-                for c in range(IN_PASSES):
-                    nc.tensor.matmul_mx(
-                        out=yT_ps[:],
-                        lhsT=wk_codes[:, c, w_cols].bitcast(FP8X4),
-                        lhsT_scale=wk_scales[:, c, w_cols],
-                        rhs=xk_codes[:, c, g, :].bitcast(FP8X4),
-                        rhs_scale=xk_scales[:, c, g, :],
-                        start=(c == 0),
-                        stop=(c == IN_PASSES - 1),
-                    )
-                nc.scalar.activation(
-                    out=yT_sb[ot][:, g, :], in_=yT_ps[:], func=ACT.Copy, accum_out=y_sums[:, ot, g : g + 1]
+            yT_ps = psum_wide.tile([P, BANK], F32, tag="wide")
+            for c in range(IN_PASSES):
+                nc.tensor.matmul_mx(
+                    out=yT_ps[:],
+                    lhsT=wk_codes[:, c, w_cols].bitcast(FP8X4),
+                    lhsT_scale=wk_scales[:, c, w_cols],
+                    rhs=xk_codes[:, c, g, :].bitcast(FP8X4),
+                    rhs_scale=xk_scales[:, c, g, :],
+                    start=(c == 0),
+                    stop=(c == IN_PASSES - 1),
                 )
+            nc.scalar.activation(
+                out=yT_sb[ot][:, g, :].rearrange("p (u r e) -> p u r e", u=2, e=2),
+                in_=yT_ps[:].rearrange("p (u e r) -> p u r e", u=2, e=2),
+                func=ACT.Copy,
+                accum_out=y_sums[:, ot, g : g + 1],
+            )
+
+        def mean_y(ot):
             scaled = work.tile([P, GROUPS], F32, tag="scaled")
             nc.scalar.activation(
                 out=scaled[:], in_=y_sums[:, ot, :], func=ACT.Copy, scale=1.0 / B, accum_out=ym[:, ot : ot + 1]
             )
 
-        def quantise_y(ot):
-            grouped = work.tile([P, GROUPS, P, PACK], BF16, tag="y_grouped", align_bytes=64)
+        def flip_y(ot):
+            y_grouped[ot] = work.tile([P, GROUPS, P, PACK], BF16, tag="y_grouped", name="yg%d" % ot, align_bytes=64)
+            grouped_words = y_grouped[ot][:].rearrange("p g o t -> p (g o t)").bitcast(F32)
+            grouped_words = grouped_words.rearrange("p (g o u) -> p g o u", g=GROUPS, u=2)
+            words = yT_sb[ot][:].rearrange("p g n -> p (g n)").bitcast(F32).rearrange("p (g w) -> p g w", g=GROUPS)
             for pair in range(GROUPS // 2):
-                flipped = psum_flip.tile([P, 2, PACK, P], BF16, tag="flip")
+                flipped = psum_flip.tile([P, 2, 2, P], F32, tag="flip")
                 for g in range(2):
-                    for t in range(PACK):
+                    for u in range(2):
                         nc.tensor.transpose(
-                            out=flipped[:, g, t, :],
-                            in_=yT_sb[ot][:, 2 * pair + g, P * t : P * (t + 1)],
-                            identity=ident_bf16[:],
+                            out=flipped[:, g, u, :],
+                            in_=words[:, 2 * pair + g, P * u : P * (u + 1)],
+                            identity=ident_f32[:],
                         )
                 nc.scalar.copy(
-                    out=grouped[:, 2 * pair : 2 * pair + 2, :, :],
-                    in_=flipped[:].rearrange("p g t o -> p g o t"),
+                    out=grouped_words[:, 2 * pair : 2 * pair + 2, :, :],
+                    in_=flipped[:].rearrange("p g u o -> p g o u"),
                 )
-            y_codes[ot] = work.tile([P, GROUPS * P], U32, tag="y_codes", name="y_codes%d" % ot, align_bytes=64)
-            y_scales[ot] = work.tile([P, GROUPS * P], U8, tag="y_scales", name="y_scales%d" % ot, align_bytes=64)
+
+        def quantise_y(ot):
+            y_codes[ot] = work.tile([P, GROUPS * P], U32, tag="y_codes", name="y_codes%d" % ot, bufs=4, align_bytes=64)
+            y_scales[ot] = work.tile([P, GROUPS * P], U8, tag="y_scales", name="y_scales%d" % ot, bufs=4, align_bytes=64)
             nc.vector.quantize_mx(
                 out=y_codes[ot][:].bitcast(FP8X4),
                 scales=y_scales[ot][:],
-                in_=grouped[:].rearrange("p g o t -> p (g o t)"),
+                in_=y_grouped[ot][:].rearrange("p g o t -> p (g o t)"),
             )
 
-        def start_base(ot):
-            base[ot] = result.tile([P, IN], F32, tag="base", name="base%d" % ot)
-            nc.vector.tensor_tensor(out=base[ot][:], in0=wa_sb[:, ot, :], in1=xm_all[:], op=ALU.mult)
-            nc.vector.tensor_tensor(out=base[ot][:], in0=base[ot][:], in1=wd_sb[:, ot, :], op=ALU.add)
+        def base_product(ot):
+            if ot % 2 == 0:
+                pair = slots.tile([P, 2, IN], F32, tag="slot", name="base%d" % ot)
+                base[ot], base[ot + 1] = pair[:, 0, :], pair[:, 1, :]
+            nc.vector.tensor_tensor(out=base[ot], in0=wa_sb[:, ot, :], in1=xm_all[:], op=ALU.mult)
 
-        def finish_base(ot):
+        def base_add(ot):
+            nc.vector.tensor_tensor(out=base[ot], in0=base[ot], in1=wd_sb[:, ot, :], op=ALU.add)
+
+        def base_mean(ot):
             nc.vector.scalar_tensor_tensor(
-                out=base[ot][:],
+                out=base[ot],
                 in0=wb_sb[:, ot, :],
                 scalar=ym[:, ot : ot + 1],
-                in1=base[ot][:],
+                in1=base[ot],
                 op0=ALU.mult,
                 op1=ALU.add,
             )
 
-        def second_matmul(ot):
-            for h in range(HALVES):
-                cols = slice(BANK * h, BANK * (h + 1))
-                corr_ps = psum_sum.tile([P, BANK], F32, tag="sum")
-                for g in range(GROUPS):
-                    y_cols = slice(P * g, P * (g + 1))
-                    nc.tensor.matmul_mx(
-                        out=corr_ps[:],
-                        lhsT=y_codes[ot][:, y_cols].bitcast(FP8X4),
-                        lhsT_scale=y_scales[ot][:, y_cols],
-                        rhs=xb_codes[:, g, cols].bitcast(FP8X4),
-                        rhs_scale=xb_scales[:, g, cols],
-                        start=(g == 0),
-                        stop=(g == GROUPS - 1),
-                    )
-                hebb = work.tile([P, BANK], F32, tag="hebb")
-                nc.vector.scalar_tensor_tensor(
-                    out=hebb[:], in0=corr_ps[:], scalar=1.0 / B, in1=wc_sb[:, ot, cols], op0=ALU.mult, op1=ALU.mult
-                )
-                nc.vector.tensor_tensor(out=base[ot][:, cols], in0=hebb[:], in1=base[ot][:, cols], op=ALU.add)
-                nc.sync.dma_start(out=out_tiles[:, ot, cols], in_=base[ot][:, cols])
+        corr_ps = {}
 
-        first_matmul(0)
-        start_base(0)
-        for ot in range(OUT_TILES):
-            quantise_y(ot)
-            if ot + 1 < OUT_TILES:
-                first_matmul(ot + 1)
-            finish_base(ot)
-            if ot + 1 < OUT_TILES:
-                start_base(ot + 1)
-            if ot >= 1:
-                second_matmul(ot - 1)
-        second_matmul(OUT_TILES - 1)
+        def second_matmul(ot, h):
+            cols = slice(BANK * h, BANK * (h + 1))
+            corr_ps[ot, h] = psum_sum.tile([P, BANK], F32, tag="sum", name="corr%d_%d" % (ot, h))
+            for g in range(GROUPS):
+                y_cols = slice(P * g, P * (g + 1))
+                nc.tensor.matmul_mx(
+                    out=corr_ps[ot, h][:],
+                    lhsT=y_codes[ot][:, y_cols].bitcast(FP8X4),
+                    lhsT_scale=y_scales[ot][:, y_cols],
+                    rhs=xb_codes[:, g, cols].bitcast(FP8X4),
+                    rhs_scale=xb_scales[:, g, cols],
+                    start=(g == 0),
+                    stop=(g == GROUPS - 1),
+                )
+
+        def scale_corr(ot, h):
+            cols = slice(BANK * h, BANK * (h + 1))
+            hebb[ot, h] = work.tile([P, BANK], F32, tag="hebb", name="hebb%d_%d" % (ot, h))
+            nc.vector.scalar_tensor_tensor(
+                out=hebb[ot, h][:],
+                in0=corr_ps[ot, h][:],
+                scalar=1.0 / B,
+                in1=wc_sb[:, ot, cols],
+                op0=ALU.mult,
+                op1=ALU.mult,
+            )
+
+        def finish(ot, h):
+            cols = slice(BANK * h, BANK * (h + 1))
+            nc.vector.tensor_tensor(out=base[ot][:, cols], in0=hebb[ot, h][:], in1=base[ot][:, cols], op=ALU.add)
+            nc.sync.dma_start(out=out_tiles[:, ot, cols], in_=base[ot][:, cols])
+
+        xk = [None] * IN_PASSES
+        xb = [None] * HALVES
+        for c in range(IN_PASSES):
+            xb[c] = group_batch_on_vector(0, c)
+            xk[c] = group_features(x_sb[0][:], c)
+        quantise_x_batch(0, 0, xb[0])
+        quantise_x_features(0, 0, xk[0])
+        quantise_x_batch(0, 1, xb[1])
+        quantise_x_features(0, 1, xk[1])
+        add_to_xm(0)
+        quantise_weight(0)
+        for g in range(1, GROUPS):
+            if g == GROUPS - 1:
+                add_to_xm(g)
+                nc.vector.reduce_sum(out=xm_col[:], in_=xm_ps[:].rearrange("p g j -> p j g"), axis=mybir.AxisListType.X)
+            if g < GROUPS - 1:
+                xb[0] = group_batch_on_vector(g, 0)
+            xk = [group_features(x_sb[g][:], c) for c in range(IN_PASSES)]
+            quantise_x_features(g, 0, xk[0])
+            if g < GROUPS - 1:
+                xb[1] = group_batch_on_vector(g, 1)
+                quantise_x_batch(g, 0, xb[0])
+            quantise_x_features(g, 1, xk[1])
+            if g < GROUPS - 1:
+                quantise_x_batch(g, 1, xb[1])
+            first_matmul(0, g - 1)
+            if g < GROUPS - 1:
+                add_to_xm(g)
+            else:
+                spread_xm()
+        first_matmul(0, GROUPS - 1)
+        mean_y(0)
+
+        LAG = 2
+        base_plan = [[0, 1], [2, 3], [4], [5], [6], [7]]
+        for s in range(OUT_TILES + LAG):
+            base_now = base_plan[s] if s < len(base_plan) else []
+            if s >= 1 and s < OUT_TILES:
+                for g in range(GROUPS):
+                    first_matmul(s, g)
+                mean_y(s)
+            if s == 3:
+                quantise_weight(1)
+            last_group = []
+            if s == 0:
+                last_group = [group_batch_on_scalar(GROUPS - 1, h) for h in range(HALVES)]
+            m = s - LAG
+            if m >= 0:
+                for h in range(HALVES):
+                    second_matmul(m, h)
+            if s < OUT_TILES:
+                flip_y(s)
+            for ot in base_now:
+                base_product(ot)
+            if m >= 0:
+                for h in range(HALVES):
+                    scale_corr(m, h)
+            for ot in base_now:
+                base_add(ot)
+            if s >= 1 and s <= OUT_TILES:
+                base_mean(s - 1)
+            if m >= 0:
+                for h in range(HALVES):
+                    finish(m, h)
+            for h, tile in enumerate(last_group):
+                quantise_x_batch(GROUPS - 1, h, tile)
+            if s < OUT_TILES:
+                quantise_y(s)

@@ -190,6 +190,14 @@ def tile_hebbianlinear_pa_kernel(tc, x, wa, wb, wc, wd, weight, out):
                     )
                 nc.scalar.copy(out=xm_all[:, BANK * h : BANK * (h + 1)], in_=spread[:])
 
+        idle_rows = keep.tile([P, BANK], BF16)
+        nc.vector.memset(idle_rows[:], 0.0)
+
+        def keep_warm(count):
+            for i in range(count):
+                bank = psum_flip.tile([P, BANK], F32, tag="flip", name="warm_bank")
+                nc.tensor.matmul(out=bank[:], lhsT=idle_rows[:, 0:P], rhs=idle_rows[:], start=True, stop=True)
+
         y_sums = keep.tile([P, OUT_TILES, GROUPS], F32)
         ym = keep.tile([P, OUT_TILES], F32)
         yT_sb = {}
@@ -308,30 +316,37 @@ def tile_hebbianlinear_pa_kernel(tc, x, wa, wb, wc, wd, weight, out):
             nc.vector.tensor_tensor(out=base[ot][:, cols], in0=hebb[ot, h][:], in1=base[ot][:, cols], op=ALU.add)
             nc.sync.dma_start(out=out_tiles[:, ot, cols], in_=base[ot][:, cols])
 
+        on_vector = ((0, 0), (0, 1), (1, 0), (1, 1), (2, 0), (2, 1),)
+        on_scalar = {0: [(3, 0), (3, 1)]}
         xk = [None] * IN_PASSES
-        xb = [None] * HALVES
+        xb = {}
+        keep_warm(6)
         for c in range(IN_PASSES):
-            xb[c] = group_batch_on_vector(0, c)
+            if (0, c) in on_vector:
+                xb[c] = group_batch_on_vector(0, c)
             xk[c] = group_features(x_sb[0][:], c)
-        quantise_x_batch(0, 0, xb[0])
-        quantise_x_features(0, 0, xk[0])
-        quantise_x_batch(0, 1, xb[1])
-        quantise_x_features(0, 1, xk[1])
+        for c in range(IN_PASSES):
+            if (0, c) in on_vector:
+                quantise_x_batch(0, c, xb[c])
+            quantise_x_features(0, c, xk[c])
         add_to_xm(0)
+        keep_warm(2)
         quantise_weight(0)
         for g in range(1, GROUPS):
+            keep_warm(2)
             if g == GROUPS - 1:
                 add_to_xm(g)
                 nc.vector.reduce_sum(out=xm_col[:], in_=xm_ps[:].rearrange("p g j -> p j g"), axis=mybir.AxisListType.X)
-            if g < GROUPS - 1:
+            if (g, 0) in on_vector:
                 xb[0] = group_batch_on_vector(g, 0)
             xk = [group_features(x_sb[g][:], c) for c in range(IN_PASSES)]
             quantise_x_features(g, 0, xk[0])
-            if g < GROUPS - 1:
+            if (g, 1) in on_vector:
                 xb[1] = group_batch_on_vector(g, 1)
+            if (g, 0) in on_vector:
                 quantise_x_batch(g, 0, xb[0])
             quantise_x_features(g, 1, xk[1])
-            if g < GROUPS - 1:
+            if (g, 1) in on_vector:
                 quantise_x_batch(g, 1, xb[1])
             first_matmul(0, g - 1)
             if g < GROUPS - 1:
@@ -345,15 +360,14 @@ def tile_hebbianlinear_pa_kernel(tc, x, wa, wb, wc, wd, weight, out):
         base_plan = [[0, 1], [2, 3], [4], [5], [6], [7]]
         for s in range(OUT_TILES + LAG):
             base_now = base_plan[s] if s < len(base_plan) else []
+            todo = on_scalar.get(s, [])
             if s >= 1 and s < OUT_TILES:
                 for g in range(GROUPS):
                     first_matmul(s, g)
                 mean_y(s)
             if s == 3:
                 quantise_weight(1)
-            last_group = []
-            if s == 0:
-                last_group = [group_batch_on_scalar(GROUPS - 1, h) for h in range(HALVES)]
+            tiles = [group_batch_on_scalar(g, h) for g, h in todo]
             m = s - LAG
             if m >= 0:
                 for h in range(HALVES):
@@ -372,7 +386,7 @@ def tile_hebbianlinear_pa_kernel(tc, x, wa, wb, wc, wd, weight, out):
             if m >= 0:
                 for h in range(HALVES):
                     finish(m, h)
-            for h, tile in enumerate(last_group):
-                quantise_x_batch(GROUPS - 1, h, tile)
+            for (g, h), tile in zip(todo, tiles):
+                quantise_x_batch(g, h, tile)
             if s < OUT_TILES:
                 quantise_y(s)

@@ -205,6 +205,7 @@ def tile_hebbianlinear_pa_kernel(tc, x, wa, wb, wc, wd, weight, out):
         y_codes = {}
         y_scales = {}
         base = {}
+        pairs = {}
         hebb = {}
 
         def first_matmul(ot, g):
@@ -264,13 +265,17 @@ def tile_hebbianlinear_pa_kernel(tc, x, wa, wb, wc, wd, weight, out):
             )
 
         def base_product(ot):
-            if ot % 2 == 0:
-                pair = slots.tile([P, 2, IN], F32, tag="slot", name="base%d" % ot)
-                base[ot], base[ot + 1] = pair[:, 0, :], pair[:, 1, :]
-            nc.vector.tensor_tensor(out=base[ot], in0=wa_sb[:, ot, :], in1=xm_all[:], op=ALU.mult)
+            pairs[ot] = slots.tile([P, 2, IN], F32, tag="slot", name="base%d" % ot)
+            base[ot], base[ot + 1] = pairs[ot][:, 0, :], pairs[ot][:, 1, :]
+            nc.vector.tensor_tensor(
+                out=pairs[ot][:],
+                in0=wa_sb[:, ot : ot + 2, :],
+                in1=xm_all[:].unsqueeze(1).to_broadcast([P, 2, IN]),
+                op=ALU.mult,
+            )
 
         def base_add(ot):
-            nc.vector.tensor_tensor(out=base[ot], in0=base[ot], in1=wd_sb[:, ot, :], op=ALU.add)
+            nc.vector.tensor_tensor(out=pairs[ot][:], in0=pairs[ot][:], in1=wd_sb[:, ot : ot + 2, :], op=ALU.add)
 
         def base_mean(ot):
             nc.vector.scalar_tensor_tensor(
@@ -301,9 +306,10 @@ def tile_hebbianlinear_pa_kernel(tc, x, wa, wb, wc, wd, weight, out):
 
         def scale_corr(ot, h):
             cols = slice(BANK * h, BANK * (h + 1))
-            hebb[ot, h] = work.tile([P, BANK], F32, tag="hebb", name="hebb%d_%d" % (ot, h))
+            if h == 0:
+                hebb[ot] = work.tile([P, IN], F32, tag="hebb", name="hebb%d" % ot)
             nc.vector.scalar_tensor_tensor(
-                out=hebb[ot, h][:],
+                out=hebb[ot][:, cols],
                 in0=corr_ps[ot, h][:],
                 scalar=1.0 / B,
                 in1=wc_sb[:, ot, cols],
@@ -311,9 +317,8 @@ def tile_hebbianlinear_pa_kernel(tc, x, wa, wb, wc, wd, weight, out):
                 op1=ALU.mult,
             )
 
-        def finish(ot, h):
-            cols = slice(BANK * h, BANK * (h + 1))
-            nc.vector.tensor_tensor(out=base[ot][:, cols], in0=hebb[ot, h][:], in1=base[ot][:, cols], op=ALU.add)
+        def finish(ot, cols):
+            nc.vector.tensor_tensor(out=base[ot][:, cols], in0=hebb[ot][:, cols], in1=base[ot][:, cols], op=ALU.add)
             nc.sync.dma_start(out=out_tiles[:, ot, cols], in_=base[ot][:, cols])
 
         on_vector = ((0, 0), (0, 1), (1, 0), (1, 1), (2, 0), (2, 1),)
@@ -357,7 +362,7 @@ def tile_hebbianlinear_pa_kernel(tc, x, wa, wb, wc, wd, weight, out):
         mean_y(0)
 
         LAG = 2
-        base_plan = [[0, 1], [2, 3], [4], [5], [6], [7]]
+        base_plan = [[0], [2], [4], [], [6]]
         for s in range(OUT_TILES + LAG):
             base_now = base_plan[s] if s < len(base_plan) else []
             todo = on_scalar.get(s, [])
@@ -384,8 +389,11 @@ def tile_hebbianlinear_pa_kernel(tc, x, wa, wb, wc, wd, weight, out):
             if s >= 1 and s <= OUT_TILES:
                 base_mean(s - 1)
             if m >= 0:
-                for h in range(HALVES):
-                    finish(m, h)
+                if m < OUT_TILES - 1:
+                    finish(m, slice(0, IN))
+                else:
+                    for h in range(HALVES):
+                        finish(m, slice(BANK * h, BANK * (h + 1)))
             for (g, h), tile in zip(todo, tiles):
                 quantise_x_batch(g, h, tile)
             if s < OUT_TILES:

@@ -13,12 +13,13 @@ P = 128
 PACK = 4
 K_PASS = P * PACK
 BANK = 512
-QUARTER = BANK // 2
 
 B, IN, OUT = 2048, 1024, 1024
 GROUPS = B // K_PASS
 IN_PASSES = IN // K_PASS
 OUT_TILES = OUT // P
+W_PARTS = OUT_TILES // PACK
+QUARTER = IN // 4
 HALVES = IN // BANK
 
 FLOPS = 2 * B * IN * OUT * 2
@@ -29,7 +30,7 @@ def tile_hebbianlinear_pa_kernel(tc, x, wa, wb, wc, wd, weight, out):
 
     with (
         tc.tile_pool(name="keep", bufs=1) as keep,
-        tc.tile_pool(name="stage", bufs=3) as stage,
+        tc.tile_pool(name="stage", bufs=4) as stage,
         tc.tile_pool(name="slots", bufs=GROUPS) as slots,
         tc.tile_pool(name="work", bufs=2) as work,
         tc.psum_pool(name="psum_wide", bufs=4) as psum_wide,
@@ -41,7 +42,7 @@ def tile_hebbianlinear_pa_kernel(tc, x, wa, wb, wc, wd, weight, out):
         make_identity(nc, ident_f32[:])
         ident_bf16 = keep.tile([P, P], BF16)
         make_identity(nc, ident_bf16[:])
-        one_over_b = keep.tile([P, 1], BF16)
+        one_over_b = keep.tile([P, 32], BF16)
         nc.vector.memset(one_over_b[:], 1.0 / B)
 
         x_rows = x.rearrange("(g p t) k -> g p t k", p=P, t=PACK)
@@ -82,101 +83,100 @@ def tile_hebbianlinear_pa_kernel(tc, x, wa, wb, wc, wd, weight, out):
             load_tiles(sb, dram, half)
         out_tiles = out.rearrange("(p ot) i -> p ot i", ot=OUT_TILES)
 
-        xk_codes = keep.tile([P, IN_PASSES, GROUPS, K_PASS], U32, align_bytes=64)
-        xk_scales = keep.tile([P, IN_PASSES, GROUPS, K_PASS], U8, align_bytes=64)
-        wk_codes = keep.tile([P, IN_PASSES, OUT], U32, align_bytes=64)
-        wk_scales = keep.tile([P, IN_PASSES, OUT], U8, align_bytes=64)
+        xk_codes = keep.tile([P, GROUPS, IN_PASSES, K_PASS], U32, align_bytes=64)
+        xk_scales = keep.tile([P, GROUPS, IN_PASSES, K_PASS], U8, align_bytes=64)
+        wk_codes = keep.tile([P, W_PARTS, IN_PASSES, K_PASS], U32, align_bytes=64)
+        wk_scales = keep.tile([P, W_PARTS, IN_PASSES, K_PASS], U8, align_bytes=64)
         xb_codes = keep.tile([P, GROUPS, IN], U32, align_bytes=64)
         xb_scales = keep.tile([P, GROUPS, IN], U8, align_bytes=64)
 
-        def group_features(rows_sb, c):
+        def stage_tile(name):
+            return stage.tile([P, PACK * IN], BF16, tag="grouped", name=name, align_bytes=64)
+
+        def group_features(rows_sb):
             words = rows_sb.bitcast(F32).rearrange("p (s w) -> p s w", s=PACK)
-            grouped = stage.tile([P, PACK * K_PASS], BF16, tag="grouped", align_bytes=64)
-            grouped_words = grouped[:].bitcast(F32).rearrange("p (s r u) -> p s r u", s=PACK, u=2)
-            for pair in range(2):
-                flipped = psum_wide.tile([P, 2, 2, P], F32, tag="wide")
-                for u in range(2):
-                    for s in range(2):
-                        first = (K_PASS // 2) * c + P * u
-                        nc.tensor.transpose(
-                            out=flipped[:, u, s, :],
-                            in_=words[:, 2 * pair + s, first : first + P],
-                            identity=ident_f32[:],
-                        )
-                nc.scalar.copy(
-                    out=grouped_words[:, 2 * pair : 2 * pair + 2, :, :],
-                    in_=flipped[:].rearrange("p u s r -> p s r u"),
-                )
+            grouped = stage_tile("features")
+            grouped_words = grouped[:].bitcast(F32).rearrange("p (c s r u) -> p c s r u", c=IN_PASSES, s=PACK, u=2)
+            for c in range(IN_PASSES):
+                for pair in range(2):
+                    flipped = psum_wide.tile([P, 2, 2, P], F32, tag="wide")
+                    for u in range(2):
+                        for s in range(2):
+                            first = (K_PASS // 2) * c + P * u
+                            nc.tensor.transpose(
+                                out=flipped[:, u, s, :],
+                                in_=words[:, 2 * pair + s, first : first + P],
+                                identity=ident_f32[:],
+                            )
+                    nc.scalar.copy(
+                        out=grouped_words[:, c, 2 * pair : 2 * pair + 2, :, :],
+                        in_=flipped[:].rearrange("p u s r -> p s r u"),
+                    )
             return grouped
 
-        def quantise_x_features(g, c, grouped):
+        def quantise_x_features(g, grouped):
             nc.vector.quantize_mx(
-                out=xk_codes[:, c, g, :].bitcast(FP8X4), scales=xk_scales[:, c, g, :], in_=grouped[:]
+                out=xk_codes[:, g, :, :].rearrange("p c n -> p (c n)").bitcast(FP8X4),
+                scales=xk_scales[:, g, :, :].rearrange("p c n -> p (c n)"),
+                in_=grouped[:],
             )
 
-        def quantise_weight(four):
-            cols = slice(K_PASS * four, K_PASS * (four + 1))
-            rows = w_sb[:, PACK * four : PACK * (four + 1), :].rearrange("p s k -> p (s k)")
-            grouped = [group_features(rows, c) for c in range(IN_PASSES)]
-            for c in range(IN_PASSES):
-                nc.vector.quantize_mx(
-                    out=wk_codes[:, c, cols].bitcast(FP8X4), scales=wk_scales[:, c, cols], in_=grouped[c][:]
-                )
+        def group_weight(part):
+            return group_features(w_sb[:, PACK * part : PACK * (part + 1), :].rearrange("p s k -> p (s k)"))
 
-        def batch_tile():
-            return stage.tile([P, PACK * BANK], BF16, tag="xb_grouped", name="xb_grouped", bufs=2, align_bytes=64)
+        def quantise_weight(part, grouped):
+            nc.vector.quantize_mx(
+                out=wk_codes[:, part, :, :].rearrange("p c n -> p (c n)").bitcast(FP8X4),
+                scales=wk_scales[:, part, :, :].rearrange("p c n -> p (c n)"),
+                in_=grouped[:],
+            )
 
-        def group_batch_on_vector(g, h):
+        def group_batch_on_vector(g, h, grouped):
             rows = x_sb[g][:].rearrange("p (t i) -> p t i", t=PACK)[:, :, BANK * h : BANK * (h + 1)]
-            grouped = batch_tile()
             nc.vector.tensor_copy(
-                out=grouped[:].rearrange("p (n i t) -> p n t i", i=4, t=PACK),
+                out=grouped[:, PACK * BANK * h : PACK * BANK * (h + 1)].rearrange("p (n i t) -> p n t i", i=4, t=PACK),
                 in_=rows.rearrange("p t (n i) -> p n t i", i=4),
             )
-            return grouped
 
-        def group_batch_on_scalar(g, h):
-            grouped = batch_tile()
-            for q in range(2):
-                bank = psum_flip.tile([P, PACK, QUARTER], BF16, tag="flip", name="rows_bank")
-                for t in range(PACK):
-                    first = IN * t + BANK * h + QUARTER * q
-                    nc.tensor.matmul(
-                        out=bank[:, t, :],
-                        lhsT=ident_bf16[:],
-                        rhs=x_sb[g][:, first : first + QUARTER],
-                        start=True,
-                        stop=True,
-                    )
-                nc.scalar.copy(
-                    out=grouped[:, PACK * QUARTER * q : PACK * QUARTER * (q + 1)].rearrange(
-                        "p (i t) -> p i t", t=PACK
-                    ),
-                    in_=bank[:].rearrange("p t i -> p i t"),
+        def group_batch_on_scalar(g, q, grouped):
+            bank = psum_sum.tile([P, PACK, QUARTER], BF16, tag="sum", name="rows_bank")
+            for t in range(PACK):
+                first = IN * t + QUARTER * q
+                nc.tensor.matmul(
+                    out=bank[:, t, :],
+                    lhsT=ident_bf16[:],
+                    rhs=x_sb[g][:, first : first + QUARTER],
+                    start=True,
+                    stop=True,
                 )
-            return grouped
-
-        def quantise_x_batch(g, h, grouped):
-            cols = slice(BANK * h, BANK * (h + 1))
-            nc.vector.quantize_mx(
-                out=xb_codes[:, g, cols].bitcast(FP8X4), scales=xb_scales[:, g, cols], in_=grouped[:]
+            nc.scalar.copy(
+                out=grouped[:, PACK * QUARTER * q : PACK * QUARTER * (q + 1)].rearrange("p (i t) -> p i t", t=PACK),
+                in_=bank[:].rearrange("p t i -> p i t"),
             )
 
-        xm_ps = psum_sum.tile([P, GROUPS, IN // P], F32, tag="sum", name="xm_ps")
+        def quantise_x_batch(g, grouped):
+            nc.vector.quantize_mx(out=xb_codes[:, g, :].bitcast(FP8X4), scales=xb_scales[:, g, :], in_=grouped[:])
+
+        xm_part = keep.tile([P, GROUPS, IN // P], F32)
         xm_col = keep.tile([P, IN // P], F32)
         xm_all = keep.tile([P, IN], F32)
 
         def add_to_xm(g):
+            xm_ps = psum_sum.tile([P, IN // P, 32], F32, tag="sum", name="xm_ps%d" % g)
             for j in range(IN // P):
                 for t in range(PACK):
                     first = IN * t + P * j
                     nc.tensor.matmul(
-                        out=xm_ps[:, g, j : j + 1],
+                        out=xm_ps[:, j, :],
                         lhsT=x_sb[g][:, first : first + P],
                         rhs=one_over_b[:],
                         start=(t == 0),
                         stop=(t == PACK - 1),
                     )
+            nc.scalar.copy(out=xm_part[:, g, :], in_=xm_ps[:, :, 0])
+
+        def add_up_xm():
+            nc.vector.reduce_sum(out=xm_col[:], in_=xm_part[:].rearrange("p g j -> p j g"), axis=mybir.AxisListType.X)
 
         def spread_xm():
             for h in range(HALVES):
@@ -211,15 +211,15 @@ def tile_hebbianlinear_pa_kernel(tc, x, wa, wb, wc, wd, weight, out):
         def first_matmul(ot, g):
             if g == 0:
                 yT_sb[ot] = work.tile([P, GROUPS, K_PASS], BF16, tag="yT", name="yT%d" % ot)
-            w_cols = slice(P * ot, P * (ot + 1))
+            part, w_cols = ot // PACK, slice(P * (ot % PACK), P * (ot % PACK + 1))
             yT_ps = psum_wide.tile([P, BANK], F32, tag="wide")
             for c in range(IN_PASSES):
                 nc.tensor.matmul_mx(
                     out=yT_ps[:],
-                    lhsT=wk_codes[:, c, w_cols].bitcast(FP8X4),
-                    lhsT_scale=wk_scales[:, c, w_cols],
-                    rhs=xk_codes[:, c, g, :].bitcast(FP8X4),
-                    rhs_scale=xk_scales[:, c, g, :],
+                    lhsT=wk_codes[:, part, c, w_cols].bitcast(FP8X4),
+                    lhsT_scale=wk_scales[:, part, c, w_cols],
+                    rhs=xk_codes[:, g, c, :].bitcast(FP8X4),
+                    rhs_scale=xk_scales[:, g, c, :],
                     start=(c == 0),
                     stop=(c == IN_PASSES - 1),
                 )
@@ -236,28 +236,28 @@ def tile_hebbianlinear_pa_kernel(tc, x, wa, wb, wc, wd, weight, out):
                 out=scaled[:], in_=y_sums[:, ot, :], func=ACT.Copy, scale=1.0 / B, accum_out=ym[:, ot : ot + 1]
             )
 
-        def flip_y(ot):
-            y_grouped[ot] = work.tile([P, GROUPS, P, PACK], BF16, tag="y_grouped", name="yg%d" % ot, align_bytes=64)
+        def flip_y(ot, pair):
+            if pair == 0:
+                y_grouped[ot] = work.tile([P, GROUPS, P, PACK], BF16, tag="y_grouped", name="yg%d" % ot, align_bytes=64)
             grouped_words = y_grouped[ot][:].rearrange("p g o t -> p (g o t)").bitcast(F32)
             grouped_words = grouped_words.rearrange("p (g o u) -> p g o u", g=GROUPS, u=2)
             words = yT_sb[ot][:].rearrange("p g n -> p (g n)").bitcast(F32).rearrange("p (g w) -> p g w", g=GROUPS)
-            for pair in range(GROUPS // 2):
-                flipped = psum_flip.tile([P, 2, 2, P], F32, tag="flip")
-                for g in range(2):
-                    for u in range(2):
-                        nc.tensor.transpose(
-                            out=flipped[:, g, u, :],
-                            in_=words[:, 2 * pair + g, P * u : P * (u + 1)],
-                            identity=ident_f32[:],
-                        )
-                nc.scalar.copy(
-                    out=grouped_words[:, 2 * pair : 2 * pair + 2, :, :],
-                    in_=flipped[:].rearrange("p g u o -> p g o u"),
-                )
+            flipped = psum_flip.tile([P, 2, 2, P], F32, tag="flip")
+            for g in range(2):
+                for u in range(2):
+                    nc.tensor.transpose(
+                        out=flipped[:, g, u, :],
+                        in_=words[:, 2 * pair + g, P * u : P * (u + 1)],
+                        identity=ident_f32[:],
+                    )
+            nc.scalar.copy(
+                out=grouped_words[:, 2 * pair : 2 * pair + 2, :, :],
+                in_=flipped[:].rearrange("p g u o -> p g o u"),
+            )
 
         def quantise_y(ot):
-            y_codes[ot] = work.tile([P, GROUPS * P], U32, tag="y_codes", name="y_codes%d" % ot, bufs=4, align_bytes=64)
-            y_scales[ot] = work.tile([P, GROUPS * P], U8, tag="y_scales", name="y_scales%d" % ot, bufs=4, align_bytes=64)
+            y_codes[ot] = work.tile([P, GROUPS * P], U32, tag="y_codes", name="y_codes%d" % ot, bufs=3, align_bytes=64)
+            y_scales[ot] = work.tile([P, GROUPS * P], U8, tag="y_scales", name="y_scales%d" % ot, bufs=3, align_bytes=64)
             nc.vector.quantize_mx(
                 out=y_codes[ot][:].bitcast(FP8X4),
                 scales=y_scales[ot][:],
@@ -321,38 +321,31 @@ def tile_hebbianlinear_pa_kernel(tc, x, wa, wb, wc, wd, weight, out):
             nc.vector.tensor_tensor(out=base[ot][:, cols], in0=hebb[ot][:, cols], in1=base[ot][:, cols], op=ALU.add)
             nc.sync.dma_start(out=out_tiles[:, ot, cols], in_=base[ot][:, cols])
 
-        on_vector = ((0, 0), (0, 1), (1, 0), (1, 1), (2, 0), (2, 1),)
-        on_scalar = {0: [(3, 0), (3, 1)]}
-        xk = [None] * IN_PASSES
-        xb = {}
         keep_warm(6)
-        for c in range(IN_PASSES):
-            if (0, c) in on_vector:
-                xb[c] = group_batch_on_vector(0, c)
-            xk[c] = group_features(x_sb[0][:], c)
-        for c in range(IN_PASSES):
-            if (0, c) in on_vector:
-                quantise_x_batch(0, c, xb[c])
-            quantise_x_features(0, c, xk[c])
+        xb = {0: stage_tile("batch0")}
+        for h in range(HALVES):
+            group_batch_on_vector(0, h, xb[0])
+        xk = group_features(x_sb[0][:])
+        quantise_x_features(0, xk)
+        quantise_x_batch(0, xb[0])
         add_to_xm(0)
         keep_warm(2)
-        quantise_weight(0)
+        wk = group_weight(0)
+        quantise_weight(0, wk)
         for g in range(1, GROUPS):
             keep_warm(2)
             if g == GROUPS - 1:
                 add_to_xm(g)
-                nc.vector.reduce_sum(out=xm_col[:], in_=xm_ps[:].rearrange("p g j -> p j g"), axis=mybir.AxisListType.X)
-            if (g, 0) in on_vector:
-                xb[0] = group_batch_on_vector(g, 0)
-            xk = [group_features(x_sb[g][:], c) for c in range(IN_PASSES)]
-            quantise_x_features(g, 0, xk[0])
-            if (g, 1) in on_vector:
-                xb[1] = group_batch_on_vector(g, 1)
-            if (g, 0) in on_vector:
-                quantise_x_batch(g, 0, xb[0])
-            quantise_x_features(g, 1, xk[1])
-            if (g, 1) in on_vector:
-                quantise_x_batch(g, 1, xb[1])
+                add_up_xm()
+            else:
+                xb[g] = stage_tile("batch")
+                group_batch_on_vector(g, 0, xb[g])
+            xk = group_features(x_sb[g][:])
+            if g < GROUPS - 1:
+                group_batch_on_vector(g, 1, xb[g])
+            quantise_x_features(g, xk)
+            if g < GROUPS - 1:
+                quantise_x_batch(g, xb[g])
             first_matmul(0, g - 1)
             if g < GROUPS - 1:
                 add_to_xm(g)
@@ -362,39 +355,42 @@ def tile_hebbianlinear_pa_kernel(tc, x, wa, wb, wc, wd, weight, out):
         mean_y(0)
 
         LAG = 2
-        base_plan = [[0], [2], [4], [], [6]]
+        base_plan = {0: [0, 2], 2: [4], 4: [6]}
         for s in range(OUT_TILES + LAG):
-            base_now = base_plan[s] if s < len(base_plan) else []
-            todo = on_scalar.get(s, [])
-            if s >= 1 and s < OUT_TILES:
+            base_now = base_plan.get(s, [])
+            m = s - LAG
+            if 1 <= s < OUT_TILES:
                 for g in range(GROUPS):
                     first_matmul(s, g)
                 mean_y(s)
             if s == 3:
-                quantise_weight(1)
-            tiles = [group_batch_on_scalar(g, h) for g, h in todo]
-            m = s - LAG
+                wk = group_weight(1)
+                quantise_weight(1, wk)
+            if s == 0:
+                last = stage_tile("batch3")
+                for q in range(4):
+                    group_batch_on_scalar(GROUPS - 1, q, last)
             if m >= 0:
                 for h in range(HALVES):
                     second_matmul(m, h)
             if s < OUT_TILES:
-                flip_y(s)
+                flip_y(s, 0)
+                flip_y(s, 1)
             for ot in base_now:
                 base_product(ot)
             if m >= 0:
-                for h in range(HALVES):
-                    scale_corr(m, h)
+                scale_corr(m, 0)
+                scale_corr(m, 1)
             for ot in base_now:
                 base_add(ot)
-            if s >= 1 and s <= OUT_TILES:
+            if 1 <= s <= OUT_TILES:
                 base_mean(s - 1)
-            if m >= 0:
-                if m < OUT_TILES - 1:
-                    finish(m, slice(0, IN))
-                else:
-                    for h in range(HALVES):
-                        finish(m, slice(BANK * h, BANK * (h + 1)))
-            for (g, h), tile in zip(todo, tiles):
-                quantise_x_batch(g, h, tile)
+            if 0 <= m < OUT_TILES - 1:
+                finish(m, slice(0, IN))
+            elif m >= 0:
+                for h in range(HALVES):
+                    finish(m, slice(BANK * h, BANK * (h + 1)))
+            if s == 0:
+                quantise_x_batch(GROUPS - 1, last)
             if s < OUT_TILES:
                 quantise_y(s)

@@ -30,7 +30,7 @@ def tile_hebbianlinear_pa_kernel(tc, x, wa, wb, wc, wd, weight, out):
 
     with (
         tc.tile_pool(name="keep", bufs=1) as keep,
-        tc.tile_pool(name="stage", bufs=4) as stage,
+        tc.tile_pool(name="stage", bufs=5) as stage,
         tc.tile_pool(name="slots", bufs=GROUPS) as slots,
         tc.tile_pool(name="work", bufs=2) as work,
         tc.psum_pool(name="psum_wide", bufs=4) as psum_wide,
@@ -190,12 +190,12 @@ def tile_hebbianlinear_pa_kernel(tc, x, wa, wb, wc, wd, weight, out):
                     )
                 nc.scalar.copy(out=xm_all[:, BANK * h : BANK * (h + 1)], in_=spread[:])
 
-        idle_rows = keep.tile([P, BANK], BF16)
+        idle_rows = keep.tile([P, 2 * P], BF16)
         nc.vector.memset(idle_rows[:], 0.0)
 
         def keep_warm(count):
             for i in range(count):
-                bank = psum_flip.tile([P, BANK], F32, tag="flip", name="warm_bank")
+                bank = psum_flip.tile([P, 2 * P], F32, tag="flip", name="warm_bank")
                 nc.tensor.matmul(out=bank[:], lhsT=idle_rows[:, 0:P], rhs=idle_rows[:], start=True, stop=True)
 
         y_sums = keep.tile([P, OUT_TILES, GROUPS], F32)
@@ -321,76 +321,89 @@ def tile_hebbianlinear_pa_kernel(tc, x, wa, wb, wc, wd, weight, out):
             nc.vector.tensor_tensor(out=base[ot][:, cols], in0=hebb[ot][:, cols], in1=base[ot][:, cols], op=ALU.add)
             nc.sync.dma_start(out=out_tiles[:, ot, cols], in_=base[ot][:, cols])
 
-        keep_warm(6)
-        xb = {0: stage_tile("batch0")}
+        xk = {}
+        xb = {}
+        keep_warm(12)
+        xb[0] = stage_tile("batch0")
         for h in range(HALVES):
             group_batch_on_vector(0, h, xb[0])
-        xk = group_features(x_sb[0][:])
-        quantise_x_features(0, xk)
+        xk[0] = group_features(x_sb[0][:])
+        quantise_x_features(0, xk[0])
         quantise_x_batch(0, xb[0])
         add_to_xm(0)
-        keep_warm(2)
+        keep_warm(4)
         wk = group_weight(0)
+        keep_warm(6)
+        xb[1] = stage_tile("batch1")
+        group_batch_on_vector(1, 0, xb[1])
         quantise_weight(0, wk)
-        for g in range(1, GROUPS):
-            keep_warm(2)
-            if g == GROUPS - 1:
-                add_to_xm(g)
-                add_up_xm()
-            else:
-                xb[g] = stage_tile("batch")
-                group_batch_on_vector(g, 0, xb[g])
-            xk = group_features(x_sb[g][:])
-            if g < GROUPS - 1:
-                group_batch_on_vector(g, 1, xb[g])
-            quantise_x_features(g, xk)
-            if g < GROUPS - 1:
-                quantise_x_batch(g, xb[g])
-            first_matmul(0, g - 1)
-            if g < GROUPS - 1:
-                add_to_xm(g)
-            else:
-                spread_xm()
-        first_matmul(0, GROUPS - 1)
+        group_batch_on_vector(1, 1, xb[1])
+        xk[1] = group_features(x_sb[1][:])
+        quantise_x_features(1, xk[1])
+        add_to_xm(1)
+        keep_warm(2)
+        xk[2] = group_features(x_sb[2][:])
+        quantise_x_features(2, xk[2])
+        add_to_xm(2)
+        first_matmul(0, 0)
+        add_to_xm(3)
+        add_up_xm()
+        quantise_x_batch(1, xb[1])
+        xb[2] = stage_tile("batch2")
+        group_batch_on_vector(2, 0, xb[2])
+        xk[3] = group_features(x_sb[3][:])
+        spread_xm()
+        first_matmul(0, 1)
+        first_matmul(0, 2)
+        base_product(0)
+        quantise_x_features(3, xk[3])
+        for q in range(2, 4):
+            group_batch_on_scalar(2, q, xb[2])
+        base_add(0)
+        first_matmul(0, 3)
         mean_y(0)
+        xb[3] = stage_tile("batch3")
+        for q in range(4):
+            group_batch_on_scalar(3, q, xb[3])
+        flip_y(0, 0)
+        flip_y(0, 1)
+        quantise_x_batch(2, xb[2])
 
         LAG = 2
-        base_plan = {0: [0, 2], 2: [4], 4: [6]}
-        for s in range(OUT_TILES + LAG):
-            base_now = base_plan.get(s, [])
+        product_plan = {1: 2, 2: 4, 4: 6}
+        add_plan = {1: 2, 2: 4, 4: 6}
+        for s in range(1, OUT_TILES + LAG):
             m = s - LAG
-            if 1 <= s < OUT_TILES:
+            if s < OUT_TILES:
                 for g in range(GROUPS):
                     first_matmul(s, g)
                 mean_y(s)
-            if s == 3:
+            if s == 1:
                 wk = group_weight(1)
+            if s == 2:
                 quantise_weight(1, wk)
-            if s == 0:
-                last = stage_tile("batch3")
-                for q in range(4):
-                    group_batch_on_scalar(GROUPS - 1, q, last)
             if m >= 0:
                 for h in range(HALVES):
                     second_matmul(m, h)
             if s < OUT_TILES:
                 flip_y(s, 0)
                 flip_y(s, 1)
-            for ot in base_now:
-                base_product(ot)
+            if s in product_plan:
+                base_product(product_plan[s])
+            if s == 1:
+                quantise_x_batch(3, xb[3])
+                quantise_y(0)
             if m >= 0:
                 scale_corr(m, 0)
                 scale_corr(m, 1)
-            for ot in base_now:
-                base_add(ot)
-            if 1 <= s <= OUT_TILES:
+            if s in add_plan:
+                base_add(add_plan[s])
+            if s <= OUT_TILES:
                 base_mean(s - 1)
             if 0 <= m < OUT_TILES - 1:
                 finish(m, slice(0, IN))
             elif m >= 0:
                 for h in range(HALVES):
                     finish(m, slice(BANK * h, BANK * (h + 1)))
-            if s == 0:
-                quantise_x_batch(GROUPS - 1, last)
             if s < OUT_TILES:
                 quantise_y(s)

@@ -93,11 +93,11 @@ def tile_hebbianlinear_pa_kernel(tc, x, wa, wb, wc, wd, weight, out):
         def stage_tile(name):
             return stage.tile([P, PACK * IN], BF16, tag="grouped", name=name, align_bytes=64)
 
-        def group_features(rows_sb):
+        def group_features(rows_sb, passes=range(IN_PASSES), grouped=None):
             words = rows_sb.bitcast(F32).rearrange("p (s w) -> p s w", s=PACK)
-            grouped = stage_tile("features")
+            grouped = grouped or stage_tile("features")
             grouped_words = grouped[:].bitcast(F32).rearrange("p (c s r u) -> p c s r u", c=IN_PASSES, s=PACK, u=2)
-            for c in range(IN_PASSES):
+            for c in passes:
                 for pair in range(2):
                     flipped = psum_wide.tile([P, 2, 2, P], F32, tag="wide")
                     for u in range(2):
@@ -351,23 +351,25 @@ def tile_hebbianlinear_pa_kernel(tc, x, wa, wb, wc, wd, weight, out):
         quantise_x_batch(1, xb[1])
         xb[2] = stage_tile("batch2")
         group_batch_on_vector(2, 0, xb[2])
-        xk[3] = group_features(x_sb[3][:])
+        xk[3] = group_features(x_sb[3][:], (0,))
         spread_xm()
+        group_features(x_sb[3][:], (1,), xk[3])
         first_matmul(0, 1)
         first_matmul(0, 2)
-        base_product(0)
+        group_batch_on_vector(2, 1, xb[2])
         quantise_x_features(3, xk[3])
-        for q in range(2, 4):
-            group_batch_on_scalar(2, q, xb[2])
-        base_add(0)
+        base_product(0)
+        quantise_x_batch(2, xb[2])
+        xb[3] = stage_tile("batch3")
+        for q in range(2):
+            group_batch_on_scalar(3, q, xb[3])
         first_matmul(0, 3)
         mean_y(0)
-        xb[3] = stage_tile("batch3")
-        for q in range(4):
+        for q in range(2, 4):
             group_batch_on_scalar(3, q, xb[3])
         flip_y(0, 0)
         flip_y(0, 1)
-        quantise_x_batch(2, xb[2])
+        base_add(0)
 
         LAG = 2
         product_plan = {1: 2, 2: 4, 4: 6}

@@ -47,16 +47,14 @@ def tile_hebbianlinear_pa_kernel(tc, x, wa, wb, wc, wd, weight, out):
 
         x_rows = x.rearrange("(g p t) k -> g p t k", p=P, t=PACK)
         x_sb = [slots.tile([P, PACK * IN], BF16, tag="slot", name="x_sb%d" % g) for g in range(GROUPS)]
+        x_order = ["p (h t k) -> p t h k"] + ["p (t h k) -> p t h k"] * (GROUPS - 1)
+        x_view = [x_sb[g][:].rearrange(x_order[g], t=PACK, h=HALVES) for g in range(GROUPS)]
         w_sb = keep.tile([P, OUT_TILES, IN], BF16)
         wa_sb = keep.tile([P, OUT_TILES, IN], BF16)
         wb_sb = keep.tile([P, OUT_TILES, IN], BF16)
         wc_sb = keep.tile([P, OUT_TILES, IN], BF16)
         wd_sb = keep.tile([P, OUT_TILES, IN], BF16)
 
-        def load_x(g, cols):
-            nc.sync.dma_start(
-                out=x_sb[g][:].rearrange("p (t k) -> p t k", t=PACK)[:, :, cols], in_=x_rows[g][:, :, cols]
-            )
 
         def load_tiles(sb, dram, half):
             tiles = slice(PACK * half, PACK * (half + 1))
@@ -65,10 +63,10 @@ def tile_hebbianlinear_pa_kernel(tc, x, wa, wb, wc, wd, weight, out):
             )
 
         for h in range(HALVES):
-            load_x(0, slice(BANK * h, BANK * (h + 1)))
+            nc.sync.dma_start(out=x_view[0][:, :, h, :], in_=x_rows[0][:, :, BANK * h : BANK * (h + 1)])
         load_tiles(w_sb, weight, 0)
         for g in range(1, GROUPS):
-            load_x(g, slice(0, IN))
+            nc.sync.dma_start(out=x_sb[g][:].rearrange("p (t k) -> p t k", t=PACK), in_=x_rows[g])
         for sb, dram, half in (
             (wa_sb, wa, 0),
             (wd_sb, wd, 0),
@@ -93,8 +91,8 @@ def tile_hebbianlinear_pa_kernel(tc, x, wa, wb, wc, wd, weight, out):
         def stage_tile(name):
             return stage.tile([P, PACK * IN], BF16, tag="grouped", name=name, align_bytes=64)
 
-        def group_features(rows_sb, passes=range(IN_PASSES), grouped=None):
-            words = rows_sb.bitcast(F32).rearrange("p (s w) -> p s w", s=PACK)
+        def group_features(rows_sb, passes=range(IN_PASSES), grouped=None, order="p (s c w) -> p s c w"):
+            words = rows_sb.bitcast(F32).rearrange(order, s=PACK, c=IN_PASSES)
             grouped = grouped or stage_tile("features")
             grouped_words = grouped[:].bitcast(F32).rearrange("p (c s r u) -> p c s r u", c=IN_PASSES, s=PACK, u=2)
             for c in passes:
@@ -102,10 +100,9 @@ def tile_hebbianlinear_pa_kernel(tc, x, wa, wb, wc, wd, weight, out):
                     flipped = psum_wide.tile([P, 2, 2, P], F32, tag="wide")
                     for u in range(2):
                         for s in range(2):
-                            first = (K_PASS // 2) * c + P * u
                             nc.tensor.transpose(
                                 out=flipped[:, u, s, :],
-                                in_=words[:, 2 * pair + s, first : first + P],
+                                in_=words[:, 2 * pair + s, c, P * u : P * (u + 1)],
                                 identity=ident_f32[:],
                             )
                     nc.scalar.copy(
@@ -132,20 +129,19 @@ def tile_hebbianlinear_pa_kernel(tc, x, wa, wb, wc, wd, weight, out):
             )
 
         def group_batch_on_vector(g, h, grouped):
-            rows = x_sb[g][:].rearrange("p (t i) -> p t i", t=PACK)[:, :, BANK * h : BANK * (h + 1)]
             nc.vector.tensor_copy(
                 out=grouped[:, PACK * BANK * h : PACK * BANK * (h + 1)].rearrange("p (n i t) -> p n t i", i=4, t=PACK),
-                in_=rows.rearrange("p t (n i) -> p n t i", i=4),
+                in_=x_view[g][:, :, h, :].rearrange("p t (n i) -> p n t i", i=4),
             )
 
         def group_batch_on_scalar(g, q, grouped):
             bank = psum_sum.tile([P, PACK, QUARTER], BF16, tag="sum", name="rows_bank")
             for t in range(PACK):
-                first = IN * t + QUARTER * q
+                first = QUARTER * (q % 2)
                 nc.tensor.matmul(
                     out=bank[:, t, :],
                     lhsT=ident_bf16[:],
-                    rhs=x_sb[g][:, first : first + QUARTER],
+                    rhs=x_view[g][:, t, q // 2, first : first + QUARTER],
                     start=True,
                     stop=True,
                 )
@@ -165,10 +161,10 @@ def tile_hebbianlinear_pa_kernel(tc, x, wa, wb, wc, wd, weight, out):
             xm_ps = psum_sum.tile([P, IN // P, 32], F32, tag="sum", name="xm_ps%d" % g)
             for j in range(IN // P):
                 for t in range(PACK):
-                    first = IN * t + P * j
+                    h, first = divmod(P * j, BANK)
                     nc.tensor.matmul(
                         out=xm_ps[:, j, :],
-                        lhsT=x_sb[g][:, first : first + P],
+                        lhsT=x_view[g][:, t, h, first : first + P],
                         rhs=one_over_b[:],
                         start=(t == 0),
                         stop=(t == PACK - 1),
@@ -327,7 +323,7 @@ def tile_hebbianlinear_pa_kernel(tc, x, wa, wb, wc, wd, weight, out):
         xb[0] = stage_tile("batch0")
         for h in range(HALVES):
             group_batch_on_vector(0, h, xb[0])
-        xk[0] = group_features(x_sb[0][:])
+        xk[0] = group_features(x_sb[0][:], order="p (c s w) -> p s c w")
         quantise_x_features(0, xk[0])
         quantise_x_batch(0, xb[0])
         add_to_xm(0)

@@ -18,6 +18,7 @@ B, IN, OUT = 2048, 1024, 1024
 GROUPS = B // K_PASS
 IN_PASSES = IN // K_PASS
 OUT_TILES = OUT // P
+TENSOR_BASE = (6, 7)
 W_PARTS = OUT_TILES // PACK
 QUARTER = IN // 4
 HALVES = IN // BANK
@@ -260,28 +261,72 @@ def tile_hebbianlinear_pa_kernel(tc, x, wa, wb, wc, wd, weight, out):
                 in_=y_grouped[ot][:].rearrange("p g o t -> p (g o t)"),
             )
 
+        waT = {}
+        base_ps = {}
+
+        def flip_wa(ot):
+            bank = psum_wide.tile([P, 2, BANK // P, P], BF16, tag="wide", name="wa_bank")
+            for i in range(2):
+                for j in range(BANK // P):
+                    first = BANK + P * j
+                    nc.tensor.transpose(
+                        out=bank[:, i, j, :], in_=wa_sb[:, ot + i, first : first + P], identity=ident_bf16[:]
+                    )
+            turned = stage.tile([P, 2, BANK // P, P], F32, tag="grouped", name="waT%d" % ot, align_bytes=64)
+            for j in range(BANK // P):
+                nc.scalar.activation(
+                    out=turned[:, :, j, :],
+                    in_=bank[:, :, j, :],
+                    func=ACT.Copy,
+                    scale=xm_col[:, BANK // P + j : BANK // P + j + 1],
+                )
+            waT[ot], waT[ot + 1] = turned[:, 0, :, :], turned[:, 1, :, :]
+
+        def base_by_tensor(ot):
+            base_ps[ot] = psum_wide.tile([P, BANK], F32, tag="wide", name="base_ps%d" % ot)
+            nc.tensor.matmul(
+                out=base_ps[ot][:], lhsT=ident_bf16[:], rhs=wd_sb[:, ot, BANK:IN], start=True, stop=False
+            )
+            for j in range(BANK // P):
+                nc.tensor.matmul(
+                    out=base_ps[ot][:, P * j : P * (j + 1)],
+                    lhsT=waT[ot][:, j, :],
+                    rhs=ident_f32[:],
+                    is_transpose=True,
+                    start=False,
+                    stop=(j == BANK // P - 1),
+                )
+
         def base_product(ot):
+            cols = slice(0, BANK if ot in TENSOR_BASE else IN)
             pairs[ot] = slots.tile([P, 2, IN], F32, tag="slot", name="base%d" % ot)
             base[ot], base[ot + 1] = pairs[ot][:, 0, :], pairs[ot][:, 1, :]
             nc.vector.tensor_tensor(
-                out=pairs[ot][:],
-                in0=wa_sb[:, ot : ot + 2, :],
-                in1=xm_all[:].unsqueeze(1).to_broadcast([P, 2, IN]),
+                out=pairs[ot][:, :, cols],
+                in0=wa_sb[:, ot : ot + 2, cols],
+                in1=xm_all[:, cols].unsqueeze(1).to_broadcast([P, 2, cols.stop]),
                 op=ALU.mult,
             )
 
         def base_add(ot):
-            nc.vector.tensor_tensor(out=pairs[ot][:], in0=pairs[ot][:], in1=wd_sb[:, ot : ot + 2, :], op=ALU.add)
+            cols = slice(0, BANK if ot in TENSOR_BASE else IN)
+            nc.vector.tensor_tensor(
+                out=pairs[ot][:, :, cols], in0=pairs[ot][:, :, cols], in1=wd_sb[:, ot : ot + 2, cols], op=ALU.add
+            )
 
         def base_mean(ot):
-            nc.vector.scalar_tensor_tensor(
-                out=base[ot],
-                in0=wb_sb[:, ot, :],
-                scalar=ym[:, ot : ot + 1],
-                in1=base[ot],
-                op0=ALU.mult,
-                op1=ALU.add,
-            )
+            parts = [(slice(0, IN), base[ot])]
+            if ot in TENSOR_BASE:
+                parts = [(slice(BANK, IN), base_ps[ot][:]), (slice(0, BANK), base[ot][:, 0:BANK])]
+            for cols, so_far in parts:
+                nc.vector.scalar_tensor_tensor(
+                    out=base[ot][:, cols],
+                    in0=wb_sb[:, ot, cols],
+                    scalar=ym[:, ot : ot + 1],
+                    in1=so_far,
+                    op0=ALU.mult,
+                    op1=ALU.add,
+                )
 
         corr_ps = {}
 
@@ -319,7 +364,7 @@ def tile_hebbianlinear_pa_kernel(tc, x, wa, wb, wc, wd, weight, out):
 
         xk = {}
         xb = {}
-        keep_warm(12)
+        keep_warm(8)
         xb[0] = stage_tile("batch0")
         for h in range(HALVES):
             group_batch_on_vector(0, h, xb[0])
@@ -386,6 +431,12 @@ def tile_hebbianlinear_pa_kernel(tc, x, wa, wb, wc, wd, weight, out):
             if s < OUT_TILES:
                 flip_y(s, 0)
                 flip_y(s, 1)
+                if s in TENSOR_BASE:
+                    base_by_tensor(s)
+                if s + 1 in TENSOR_BASE and s % 2 == 1:
+                    flip_wa(s + 1)
+            if s - 1 in TENSOR_BASE:
+                base_mean(s - 1)
             if s in product_plan:
                 base_product(product_plan[s])
             if s == 1:
@@ -396,7 +447,7 @@ def tile_hebbianlinear_pa_kernel(tc, x, wa, wb, wc, wd, weight, out):
                 scale_corr(m, 1)
             if s in add_plan:
                 base_add(add_plan[s])
-            if s <= OUT_TILES:
+            if s <= OUT_TILES and s - 1 not in TENSOR_BASE:
                 base_mean(s - 1)
             if 0 <= m < OUT_TILES - 1:
                 finish(m, slice(0, IN))

@@ -364,7 +364,7 @@ def tile_hebbianlinear_pa_kernel(tc, x, wa, wb, wc, wd, weight, out):
 
         xk = {}
         xb = {}
-        keep_warm(8)
+        keep_warm(12)
         xb[0] = stage_tile("batch0")
         for h in range(HALVES):
             group_batch_on_vector(0, h, xb[0])

@@ -43,7 +43,7 @@ def tile_hebbianlinear_pa_kernel(tc, x, wa, wb, wc, wd, weight, out):
         make_identity(nc, ident_f32[:])
         ident_bf16 = keep.tile([P, P], BF16)
         make_identity(nc, ident_bf16[:])
-        one_over_b = keep.tile([P, 32], BF16)
+        one_over_b = keep.tile([P, 48], BF16)
         nc.vector.memset(one_over_b[:], 1.0 / B)
 
         x_rows = x.rearrange("(g p t) k -> g p t k", p=P, t=PACK)
@@ -159,7 +159,7 @@ def tile_hebbianlinear_pa_kernel(tc, x, wa, wb, wc, wd, weight, out):
         xm_all = keep.tile([P, IN], F32)
 
         def add_to_xm(g):
-            xm_ps = psum_sum.tile([P, IN // P, 32], F32, tag="sum", name="xm_ps%d" % g)
+            xm_ps = psum_sum.tile([P, IN // P, 48], F32, tag="sum", name="xm_ps%d" % g)
             for j in range(IN // P):
                 for t in range(PACK):
                     h, first = divmod(P * j, BANK)
@@ -413,8 +413,8 @@ def tile_hebbianlinear_pa_kernel(tc, x, wa, wb, wc, wd, weight, out):
         base_add(0)
 
         LAG = 2
-        product_plan = {1: 2, 2: 4, 4: 6}
-        add_plan = {1: 2, 2: 4, 4: 6}
+        product_plan = {1: 2, 3: 4, 5: 6}
+        add_plan = {1: 2, 3: 4, 5: 6}
         for s in range(1, OUT_TILES + LAG):
             m = s - LAG
             if s < OUT_TILES:
@@ -435,7 +435,7 @@ def tile_hebbianlinear_pa_kernel(tc, x, wa, wb, wc, wd, weight, out):
                     base_by_tensor(s)
                 if s + 1 in TENSOR_BASE and s % 2 == 1:
                     flip_wa(s + 1)
-            if s - 1 in TENSOR_BASE:
+            if s - 1 in TENSOR_BASE and s < OUT_TILES:
                 base_mean(s - 1)
             if s in product_plan:
                 base_product(product_plan[s])
@@ -447,7 +447,7 @@ def tile_hebbianlinear_pa_kernel(tc, x, wa, wb, wc, wd, weight, out):
                 scale_corr(m, 1)
             if s in add_plan:
                 base_add(add_plan[s])
-            if s <= OUT_TILES and s - 1 not in TENSOR_BASE:
+            if s == OUT_TILES or (s < OUT_TILES and s - 1 not in TENSOR_BASE):
                 base_mean(s - 1)
             if 0 <= m < OUT_TILES - 1:
                 finish(m, slice(0, IN))

import concourse.mybir as mybir
from concourse.masks import make_identity

F32 = mybir.dt.float32
BF16 = mybir.dt.bfloat16
U32 = mybir.dt.uint32
U8 = mybir.dt.uint8
FP8X4 = mybir.dt.float8_e4m3fn_x4
ALU = mybir.AluOpType
ACT = mybir.ActivationFunctionType

P = 128
PACK = 4
K_PASS = P * PACK
BANK = 512

B, IN, OUT = 2048, 1024, 1024
GROUPS = B // K_PASS
IN_PASSES = IN // K_PASS
OUT_TILES = OUT // P
TENSOR_BASE = (6, 7)
W_PARTS = OUT_TILES // PACK
QUARTER = IN // 4
HALVES = IN // BANK

FLOPS = 2 * B * IN * OUT * 2


def tile_hebbianlinear_pa_kernel(tc, x, wa, wb, wc, wd, weight, out):
    nc = tc.nc

    with (
        tc.tile_pool(name="keep", bufs=1) as keep,
        tc.tile_pool(name="stage", bufs=5) as stage,
        tc.tile_pool(name="slots", bufs=GROUPS) as slots,
        tc.tile_pool(name="work", bufs=2) as work,
        tc.psum_pool(name="psum_wide", bufs=4) as psum_wide,
        tc.psum_pool(name="psum_flip", bufs=2) as psum_flip,
        tc.psum_pool(name="psum_sum", bufs=2) as psum_sum,
        tc.manual_schedule(),
    ):
        ident_f32 = keep.tile([P, P], F32)
        make_identity(nc, ident_f32[:])
        ident_bf16 = keep.tile([P, P], BF16)
        make_identity(nc, ident_bf16[:])
        one_over_b = keep.tile([P, 48], BF16)
        nc.vector.memset(one_over_b[:], 1.0 / B)

        x_rows = x.rearrange("(g p t) k -> g p t k", p=P, t=PACK)
        x_sb = [slots.tile([P, PACK * IN], BF16, tag="slot", name="x_sb%d" % g) for g in range(GROUPS)]
        x_order = ["p (h t k) -> p t h k"] + ["p (t h k) -> p t h k"] * (GROUPS - 1)
        x_view = [x_sb[g][:].rearrange(x_order[g], t=PACK, h=HALVES) for g in range(GROUPS)]
        w_sb = keep.tile([P, OUT_TILES, IN], BF16)
        wa_sb = keep.tile([P, OUT_TILES, IN], BF16)
        wb_sb = keep.tile([P, OUT_TILES, IN], BF16)
        wc_sb = keep.tile([P, OUT_TILES, IN], BF16)
        wd_sb = keep.tile([P, OUT_TILES, IN], BF16)


        def load_tiles(sb, dram, half):
            tiles = slice(PACK * half, PACK * (half + 1))
            nc.sync.dma_start(
                out=sb[:, tiles, :], in_=dram.rearrange("(p ot) i -> p ot i", ot=OUT_TILES)[:, tiles, :]
            )

        for h in range(HALVES):
            nc.sync.dma_start(out=x_view[0][:, :, h, :], in_=x_rows[0][:, :, BANK * h : BANK * (h + 1)])
        load_tiles(w_sb, weight, 0)
        for g in range(1, GROUPS):
            nc.sync.dma_start(out=x_sb[g][:].rearrange("p (t k) -> p t k", t=PACK), in_=x_rows[g])
        for sb, dram, half in (
            (wa_sb, wa, 0),
            (wd_sb, wd, 0),
            (w_sb, weight, 1),
            (wb_sb, wb, 0),
            (wc_sb, wc, 0),
            (wa_sb, wa, 1),
            (wd_sb, wd, 1),
            (wb_sb, wb, 1),
            (wc_sb, wc, 1),
        ):
            load_tiles(sb, dram, half)
        out_tiles = out.rearrange("(p ot) i -> p ot i", ot=OUT_TILES)

        xk_codes = keep.tile([P, GROUPS, IN_PASSES, K_PASS], U32, align_bytes=64)
        xk_scales = keep.tile([P, GROUPS, IN_PASSES, K_PASS], U8, align_bytes=64)
        wk_codes = keep.tile([P, W_PARTS, IN_PASSES, K_PASS], U32, align_bytes=64)
        wk_scales = keep.tile([P, W_PARTS, IN_PASSES, K_PASS], U8, align_bytes=64)
        xb_codes = keep.tile([P, GROUPS, IN], U32, align_bytes=64)
        xb_scales = keep.tile([P, GROUPS, IN], U8, align_bytes=64)

        def stage_tile(name):
            return stage.tile([P, PACK * IN], BF16, tag="grouped", name=name, align_bytes=64)

        def group_features(rows_sb, passes=range(IN_PASSES), grouped=None, order="p (s c w) -> p s c w"):
            words = rows_sb.bitcast(F32).rearrange(order, s=PACK, c=IN_PASSES)
            grouped = grouped or stage_tile("features")
            grouped_words = grouped[:].bitcast(F32).rearrange("p (c s r u) -> p c s r u", c=IN_PASSES, s=PACK, u=2)
            for c in passes:
                for pair in range(2):
                    flipped = psum_wide.tile([P, 2, 2, P], F32, tag="wide")
                    for u in range(2):
                        for s in range(2):
                            nc.tensor.transpose(
                                out=flipped[:, u, s, :],
                                in_=words[:, 2 * pair + s, c, P * u : P * (u + 1)],
                                identity=ident_f32[:],
                            )
                    nc.scalar.copy(
                        out=grouped_words[:, c, 2 * pair : 2 * pair + 2, :, :],
                        in_=flipped[:].rearrange("p u s r -> p s r u"),
                    )
            return grouped

        def quantise_x_features(g, grouped):
            nc.vector.quantize_mx(
                out=xk_codes[:, g, :, :].rearrange("p c n -> p (c n)").bitcast(FP8X4),
                scales=xk_scales[:, g, :, :].rearrange("p c n -> p (c n)"),
                in_=grouped[:],
            )

        def group_weight(part):
            return group_features(w_sb[:, PACK * part : PACK * (part + 1), :].rearrange("p s k -> p (s k)"))

        def quantise_weight(part, grouped):
            nc.vector.quantize_mx(
                out=wk_codes[:, part, :, :].rearrange("p c n -> p (c n)").bitcast(FP8X4),
                scales=wk_scales[:, part, :, :].rearrange("p c n -> p (c n)"),
                in_=grouped[:],
            )

        def group_batch_on_vector(g, h, grouped):
            nc.vector.tensor_copy(
                out=grouped[:, PACK * BANK * h : PACK * BANK * (h + 1)].rearrange("p (n i t) -> p n t i", i=4, t=PACK),
                in_=x_view[g][:, :, h, :].rearrange("p t (n i) -> p n t i", i=4),
            )

        def group_batch_on_scalar(g, q, grouped):
            bank = psum_sum.tile([P, PACK, QUARTER], BF16, tag="sum", name="rows_bank")
            for t in range(PACK):
                first = QUARTER * (q % 2)
                nc.tensor.matmul(
                    out=bank[:, t, :],
                    lhsT=ident_bf16[:],
                    rhs=x_view[g][:, t, q // 2, first : first + QUARTER],
                    start=True,
                    stop=True,
                )
            nc.scalar.copy(
                out=grouped[:, PACK * QUARTER * q : PACK * QUARTER * (q + 1)].rearrange("p (i t) -> p i t", t=PACK),
                in_=bank[:].rearrange("p t i -> p i t"),
            )

        def quantise_x_batch(g, grouped):
            nc.vector.quantize_mx(out=xb_codes[:, g, :].bitcast(FP8X4), scales=xb_scales[:, g, :], in_=grouped[:])

        xm_part = keep.tile([P, GROUPS, IN // P], F32)
        xm_col = keep.tile([P, IN // P], F32)
        xm_all = keep.tile([P, IN], F32)

        def add_to_xm(g):
            xm_ps = psum_sum.tile([P, IN // P, 48], F32, tag="sum", name="xm_ps%d" % g)
            for j in range(IN // P):
                for t in range(PACK):
                    h, first = divmod(P * j, BANK)
                    nc.tensor.matmul(
                        out=xm_ps[:, j, :],
                        lhsT=x_view[g][:, t, h, first : first + P],
                        rhs=one_over_b[:],
                        start=(t == 0),
                        stop=(t == PACK - 1),
                    )
            nc.scalar.copy(out=xm_part[:, g, :], in_=xm_ps[:, :, 0])

        def add_up_xm():
            nc.vector.reduce_sum(out=xm_col[:], in_=xm_part[:].rearrange("p g j -> p j g"), axis=mybir.AxisListType.X)

        def spread_xm():
            for h in range(HALVES):
                spread = psum_sum.tile([P, BANK], F32, tag="sum", name="spread%d" % h)
                for j in range(BANK // P):
                    col = (BANK // P) * h + j
                    nc.tensor.transpose(
                        out=spread[:, P * j : P * (j + 1)],
                        in_=xm_col[:, col : col + 1].to_broadcast([P, P]),
                        identity=ident_f32[:],
                    )
                nc.scalar.copy(out=xm_all[:, BANK * h : BANK * (h + 1)], in_=spread[:])

        idle_rows = keep.tile([P, 2 * P], BF16)
        nc.vector.memset(idle_rows[:], 0.0)

        def keep_warm(count):
            for i in range(count):
                bank = psum_flip.tile([P, 2 * P], F32, tag="flip", name="warm_bank")
                nc.tensor.matmul(out=bank[:], lhsT=idle_rows[:, 0:P], rhs=idle_rows[:], start=True, stop=True)

        y_sums = keep.tile([P, OUT_TILES, GROUPS], F32)
        ym = keep.tile([P, OUT_TILES], F32)
        yT_sb = {}
        y_grouped = {}
        y_codes = {}
        y_scales = {}
        base = {}
        pairs = {}
        hebb = {}

        def first_matmul(ot, g):
            if g == 0:
                yT_sb[ot] = work.tile([P, GROUPS, K_PASS], BF16, tag="yT", name="yT%d" % ot)
            part, w_cols = ot // PACK, slice(P * (ot % PACK), P * (ot % PACK + 1))
            yT_ps = psum_wide.tile([P, BANK], F32, tag="wide")
            for c in range(IN_PASSES):
                nc.tensor.matmul_mx(
                    out=yT_ps[:],
                    lhsT=wk_codes[:, part, c, w_cols].bitcast(FP8X4),
                    lhsT_scale=wk_scales[:, part, c, w_cols],
                    rhs=xk_codes[:, g, c, :].bitcast(FP8X4),
                    rhs_scale=xk_scales[:, g, c, :],
                    start=(c == 0),
                    stop=(c == IN_PASSES - 1),
                )
            nc.scalar.activation(
                out=yT_sb[ot][:, g, :].rearrange("p (u r e) -> p u r e", u=2, e=2),
                in_=yT_ps[:].rearrange("p (u e r) -> p u r e", u=2, e=2),
                func=ACT.Copy,
                accum_out=y_sums[:, ot, g : g + 1],
            )

        def mean_y(ot):
            scaled = work.tile([P, GROUPS], F32, tag="scaled")
            nc.scalar.activation(
                out=scaled[:], in_=y_sums[:, ot, :], func=ACT.Copy, scale=1.0 / B, accum_out=ym[:, ot : ot + 1]
            )

        def flip_y(ot, pair):
            if pair == 0:
                y_grouped[ot] = work.tile([P, GROUPS, P, PACK], BF16, tag="y_grouped", name="yg%d" % ot, align_bytes=64)
            grouped_words = y_grouped[ot][:].rearrange("p g o t -> p (g o t)").bitcast(F32)
            grouped_words = grouped_words.rearrange("p (g o u) -> p g o u", g=GROUPS, u=2)
            words = yT_sb[ot][:].rearrange("p g n -> p (g n)").bitcast(F32).rearrange("p (g w) -> p g w", g=GROUPS)
            flipped = psum_flip.tile([P, 2, 2, P], F32, tag="flip")
            for g in range(2):
                for u in range(2):
                    nc.tensor.transpose(
                        out=flipped[:, g, u, :],
                        in_=words[:, 2 * pair + g, P * u : P * (u + 1)],
                        identity=ident_f32[:],
                    )
            nc.scalar.copy(
                out=grouped_words[:, 2 * pair : 2 * pair + 2, :, :],
                in_=flipped[:].rearrange("p g u o -> p g o u"),
            )

        def quantise_y(ot):
            y_codes[ot] = work.tile([P, GROUPS * P], U32, tag="y_codes", name="y_codes%d" % ot, bufs=3, align_bytes=64)
            y_scales[ot] = work.tile([P, GROUPS * P], U8, tag="y_scales", name="y_scales%d" % ot, bufs=3, align_bytes=64)
            nc.vector.quantize_mx(
                out=y_codes[ot][:].bitcast(FP8X4),
                scales=y_scales[ot][:],
                in_=y_grouped[ot][:].rearrange("p g o t -> p (g o t)"),
            )

        waT = {}
        base_ps = {}

        def flip_wa(ot):
            bank = psum_wide.tile([P, 2, BANK // P, P], BF16, tag="wide", name="wa_bank")
            for i in range(2):
                for j in range(BANK // P):
                    first = BANK + P * j
                    nc.tensor.transpose(
                        out=bank[:, i, j, :], in_=wa_sb[:, ot + i, first : first + P], identity=ident_bf16[:]
                    )
            turned = stage.tile([P, 2, BANK // P, P], F32, tag="grouped", name="waT%d" % ot, align_bytes=64)
            for j in range(BANK // P):
                nc.scalar.activation(
                    out=turned[:, :, j, :],
                    in_=bank[:, :, j, :],
                    func=ACT.Copy,
                    scale=xm_col[:, BANK // P + j : BANK // P + j + 1],
                )
            waT[ot], waT[ot + 1] = turned[:, 0, :, :], turned[:, 1, :, :]

        def base_by_tensor(ot):
            base_ps[ot] = psum_wide.tile([P, BANK], F32, tag="wide", name="base_ps%d" % ot)
            nc.tensor.matmul(
                out=base_ps[ot][:], lhsT=ident_bf16[:], rhs=wd_sb[:, ot, BANK:IN], start=True, stop=False
            )
            for j in range(BANK // P):
                nc.tensor.matmul(
                    out=base_ps[ot][:, P * j : P * (j + 1)],
                    lhsT=waT[ot][:, j, :],
                    rhs=ident_f32[:],
                    is_transpose=True,
                    start=False,
                    stop=(j == BANK // P - 1),
                )

        def base_product(ot):
            cols = slice(0, BANK if ot in TENSOR_BASE else IN)
            pairs[ot] = slots.tile([P, 2, IN], F32, tag="slot", name="base%d" % ot)
            base[ot], base[ot + 1] = pairs[ot][:, 0, :], pairs[ot][:, 1, :]
            nc.vector.tensor_tensor(
                out=pairs[ot][:, :, cols],
                in0=wa_sb[:, ot : ot + 2, cols],
                in1=xm_all[:, cols].unsqueeze(1).to_broadcast([P, 2, cols.stop]),
                op=ALU.mult,
            )

        def base_add(ot):
            cols = slice(0, BANK if ot in TENSOR_BASE else IN)
            nc.vector.tensor_tensor(
                out=pairs[ot][:, :, cols], in0=pairs[ot][:, :, cols], in1=wd_sb[:, ot : ot + 2, cols], op=ALU.add
            )

        def base_mean(ot):
            parts = [(slice(0, IN), base[ot])]
            if ot in TENSOR_BASE:
                parts = [(slice(BANK, IN), base_ps[ot][:]), (slice(0, BANK), base[ot][:, 0:BANK])]
            for cols, so_far in parts:
                nc.vector.scalar_tensor_tensor(
                    out=base[ot][:, cols],
                    in0=wb_sb[:, ot, cols],
                    scalar=ym[:, ot : ot + 1],
                    in1=so_far,
                    op0=ALU.mult,
                    op1=ALU.add,
                )

        corr_ps = {}

        def second_matmul(ot, h):
            cols = slice(BANK * h, BANK * (h + 1))
            corr_ps[ot, h] = psum_sum.tile([P, BANK], F32, tag="sum", name="corr%d_%d" % (ot, h))
            for g in range(GROUPS):
                y_cols = slice(P * g, P * (g + 1))
                nc.tensor.matmul_mx(
                    out=corr_ps[ot, h][:],
                    lhsT=y_codes[ot][:, y_cols].bitcast(FP8X4),
                    lhsT_scale=y_scales[ot][:, y_cols],
                    rhs=xb_codes[:, g, cols].bitcast(FP8X4),
                    rhs_scale=xb_scales[:, g, cols],
                    start=(g == 0),
                    stop=(g == GROUPS - 1),
                )

        def scale_corr(ot, h):
            cols = slice(BANK * h, BANK * (h + 1))
            if h == 0:
                hebb[ot] = work.tile([P, IN], F32, tag="hebb", name="hebb%d" % ot)
            nc.vector.scalar_tensor_tensor(
                out=hebb[ot][:, cols],
                in0=corr_ps[ot, h][:],
                scalar=1.0 / B,
                in1=wc_sb[:, ot, cols],
                op0=ALU.mult,
                op1=ALU.mult,
            )

        def finish(ot, cols):
            nc.vector.tensor_tensor(out=base[ot][:, cols], in0=hebb[ot][:, cols], in1=base[ot][:, cols], op=ALU.add)
            nc.sync.dma_start(out=out_tiles[:, ot, cols], in_=base[ot][:, cols])

        xk = {}
        xb = {}
        keep_warm(12)
        xb[0] = stage_tile("batch0")
        for h in range(HALVES):
            group_batch_on_vector(0, h, xb[0])
        xk[0] = group_features(x_sb[0][:], order="p (c s w) -> p s c w")
        quantise_x_features(0, xk[0])
        quantise_x_batch(0, xb[0])
        add_to_xm(0)
        keep_warm(4)
        wk = group_weight(0)
        keep_warm(6)
        xb[1] = stage_tile("batch1")
        group_batch_on_vector(1, 0, xb[1])
        quantise_weight(0, wk)
        group_batch_on_vector(1, 1, xb[1])
        xk[1] = group_features(x_sb[1][:])
        quantise_x_features(1, xk[1])
        add_to_xm(1)
        keep_warm(2)
        xk[2] = group_features(x_sb[2][:])
        quantise_x_features(2, xk[2])
        add_to_xm(2)
        first_matmul(0, 0)
        add_to_xm(3)
        add_up_xm()
        quantise_x_batch(1, xb[1])
        xb[2] = stage_tile("batch2")
        group_batch_on_vector(2, 0, xb[2])
        xk[3] = group_features(x_sb[3][:], (0,))
        spread_xm()
        group_features(x_sb[3][:], (1,), xk[3])
        first_matmul(0, 1)
        first_matmul(0, 2)
        group_batch_on_vector(2, 1, xb[2])
        quantise_x_features(3, xk[3])
        base_product(0)
        quantise_x_batch(2, xb[2])
        xb[3] = stage_tile("batch3")
        for q in range(2):
            group_batch_on_scalar(3, q, xb[3])
        first_matmul(0, 3)
        mean_y(0)
        for q in range(2, 4):
            group_batch_on_scalar(3, q, xb[3])
        flip_y(0, 0)
        flip_y(0, 1)
        base_add(0)

        LAG = 2
        product_plan = {1: 2, 3: 4, 5: 6}
        add_plan = {1: 2, 3: 4, 5: 6}
        for s in range(1, OUT_TILES + LAG):
            m = s - LAG
            if s < OUT_TILES:
                for g in range(GROUPS):
                    first_matmul(s, g)
                mean_y(s)
            if s == 1:
                wk = group_weight(1)
            if s == 2:
                quantise_weight(1, wk)
            if m >= 0:
                for h in range(HALVES):
                    second_matmul(m, h)
            if s < OUT_TILES:
                flip_y(s, 0)
                flip_y(s, 1)
                if s in TENSOR_BASE:
                    base_by_tensor(s)
                if s + 1 in TENSOR_BASE and s % 2 == 1:
                    flip_wa(s + 1)
            if s - 1 in TENSOR_BASE and s < OUT_TILES:
                base_mean(s - 1)
            if s in product_plan:
                base_product(product_plan[s])
            if s == 1:
                quantise_x_batch(3, xb[3])
                quantise_y(0)
            if m >= 0:
                scale_corr(m, 0)
                scale_corr(m, 1)
            if s in add_plan:
                base_add(add_plan[s])
            if s == OUT_TILES or (s < OUT_TILES and s - 1 not in TENSOR_BASE):
                base_mean(s - 1)
            if 0 <= m < OUT_TILES - 1:
                finish(m, slice(0, IN))
            elif m >= 0:
                for h in range(HALVES):
                    finish(m, slice(BANK * h, BANK * (h + 1)))
            if s < OUT_TILES:
                quantise_y(s)
